import numpy as np
import ml_dtypes


def mxq(x, axis, fmt="e4m3"):
    dtype, down = {"e4m3": (ml_dtypes.float8_e4m3fn, 7), "e5m2": (ml_dtypes.float8_e5m2, 14)}[fmt]
    v = np.moveaxis(np.asarray(x, np.float32).astype(ml_dtypes.bfloat16).astype(np.float64), axis, -1)
    blocks = v.reshape(v.shape[:-1] + (-1, 32))
    amax = np.abs(blocks).max(-1, keepdims=True)
    byte = np.maximum(np.where(amax > 0, np.frexp(amax)[1] - 1 + 127, 0) - down, 1)
    scale = np.exp2(byte - 127.0)
    codes = (blocks / scale).astype(np.float32).astype(dtype).astype(np.float64)
    return np.moveaxis((codes * scale).reshape(v.shape), -1, axis)


WIDE = False


def mx_kscale(k):
    if not WIDE:
        return np.ones(k)
    levels = np.array([10, -10, 5, -5, 0])
    a = np.random.permutation(np.resize(levels, k // 512 * 4)).reshape(k // 512, 4)
    idx = np.arange(k)
    return np.exp2(a[idx // 512, idx % 128 // 32])


BF16 = ml_dtypes.bfloat16


def bf(x):
    return np.asarray(x, np.float32).astype(BF16)


def f64(x):
    return np.asarray(x).astype(np.float64)


B, T, D = 2, 512, 1024
EPS_DENOM = 1e-6
EPS_LN = 1e-5


def elu1(z):
    return np.where(z > 0.0, z, np.exp(np.minimum(z, 0.0)) - 1.0) + 1.0


def layernorm(x, gamma, beta):
    mu = x.mean(axis=-1, keepdims=True)
    var = ((x - mu) ** 2).mean(axis=-1, keepdims=True)
    return (x - mu) * (1.0 / np.sqrt(var + EPS_LN)) * gamma + beta


def setup_inputs():
    s, u = mx_kscale(D), mx_kscale(D)
    return {"q_feat": bf(elu1(np.random.standard_normal((B, T, D))) * s),
            "kv": bf(np.random.standard_normal((B, D, D)) * 0.45 * np.sqrt(T) / s[:, None] * u[None, :]),
            "k_sum": bf(T * (1.16 + 0.15 * np.random.standard_normal((B, D))) / s),
            "audio": bf(np.random.standard_normal((B, T, D))),
            "Wo": bf(np.random.standard_normal((D, D)) * 0.5 / np.sqrt(D) / u[None, :]),
            "bo": bf(np.random.standard_normal(D) * 0.2),
            "gamma": bf(1.0 + 0.1 * np.random.standard_normal(D)),
            "beta": bf(0.1 * np.random.standard_normal(D))}


def reference(q_feat, kv, k_sum, audio, Wo, bo, gamma, beta):
    q = f64(q_feat)
    num = mxq(q, 2, "e4m3") @ mxq(f64(kv), 1, "e4m3")
    attn = num / (q * f64(k_sum)[:, None, :] + EPS_DENOM)
    y = (mxq(attn, 2, "e4m3") @ mxq(f64(Wo), 1, "e4m3").T) + f64(bo)
    return layernorm(f64(audio) + y, f64(gamma), f64(beta))

@@ -1,0 +1,319 @@
+from contextlib import ExitStack
+
+import concourse.mybir as mybir
+from concourse.masks import make_identity
+
+F32 = mybir.dt.float32
+BF16 = mybir.dt.bfloat16
+U32 = mybir.dt.uint32
+U8 = mybir.dt.uint8
+FP8X4 = mybir.dt.float8_e4m3fn_x4
+ALU = mybir.AluOpType
+ACT = mybir.ActivationFunctionType
+
+B, T, D = 2, 512, 1024
+EPS_DENOM = 1e-6
+EPS_LN = 1e-5
+P = 128
+PACK = 4
+PAIR = 2
+HALVES = PACK // PAIR
+K_PASS = P * PACK
+PASSES = D // K_PASS
+T_BLOCKS = T // P
+ROW_BLOCKS = D // P
+BANK = 512
+O_BANKS = D // BANK
+AHEAD = 2
+FLOPS = 2 * (2 * B * T * D * D)
+
+
+def tile_linearattentionlayer_pb_kernel(tc, q_feat, kv, k_sum, audio, Wo, bo, gamma, beta, out):
+    nc = tc.nc
+    with ExitStack() as stack:
+        const = stack.enter_context(tc.tile_pool(name="const", bufs=1))
+        raw = stack.enter_context(tc.tile_pool(name="raw", bufs=3))
+        keep = stack.enter_context(tc.tile_pool(name="keep", bufs=1))
+        grouped = stack.enter_context(tc.tile_pool(name="grouped", bufs=2))
+        recips = stack.enter_context(tc.tile_pool(name="recips", bufs=3))
+        stage = stack.enter_context(tc.tile_pool(name="stage", bufs=2))
+        rows = stack.enter_context(tc.tile_pool(name="rows", bufs=6))
+        small = stack.enter_context(tc.tile_pool(name="small", bufs=4))
+        psum_tp = stack.enter_context(tc.psum_pool(name="psum_tp", bufs=2))
+        psum_num = stack.enter_context(tc.psum_pool(name="psum_num", bufs=2))
+        psum_y = stack.enter_context(tc.psum_pool(name="psum_y", bufs=2))
+        stack.enter_context(tc.manual_schedule())
+
+        ident = const.tile([P, P], F32)
+        make_identity(nc, ident[:])
+        eps_denom = const.tile([P, 1], F32)
+        nc.vector.memset(eps_denom[:], EPS_DENOM)
+        eps_ln = const.tile([P, 1], F32)
+        nc.vector.memset(eps_ln[:], EPS_LN)
+        ksum_rows = const.tile([P, PAIR * P], BF16)
+        nc.vector.memset(ksum_rows[:], 0.0)
+        vectors = (bo, gamma, beta)
+        vector_rows = const.tile([P, D], BF16)
+        nc.vector.memset(vector_rows[:], 0.0)
+        pick = const.tile([P, len(vectors), P], BF16)
+        nc.vector.memset(pick[:], 0.0)
+        for v in range(len(vectors)):
+            nc.vector.memset(pick[32 * v : 32 * v + 1, v, :], 1.0)
+
+        n_ksum_rows = B * D // (PAIR * P)
+        nc.sync.dma_start(out=ksum_rows[0:n_ksum_rows, :], in_=k_sum.rearrange("b (r c) -> (b r) c", c=PAIR * P))
+        for v in range(len(vectors)):
+            nc.sync.dma_start(out=vector_rows[32 * v : 32 * v + 1, :], in_=vectors[v].unsqueeze(0))
+        wo_raw = const.tile([P, ROW_BLOCKS, D], BF16)
+
+        def load_tokens(src):
+            token_rows = raw.tile([P, T_BLOCKS, D], BF16)
+            nc.sync.dma_start(out=token_rows[:], in_=src.rearrange("(n p) d -> p n d", p=P))
+            return token_rows
+
+        def load_kv(b, g):
+            kv_rows = raw.tile([P, PACK, D], BF16)
+            nc.sync.dma_start(
+                out=kv_rows[:].rearrange("p (u e) c -> p u (e c)", u=HALVES),
+                in_=kv[b, g * K_PASS : (g + 1) * K_PASS, :].rearrange("(u p e) c -> p u (e c)", u=HALVES, p=P),
+            )
+            return kv_rows
+
+        q_raw = [load_tokens(q_feat[0])]
+        kv_raw = [load_kv(0, 0), load_kv(0, 1), load_kv(1, 0)]
+
+        spread = []
+        for v in range(len(vectors)):
+            bank_pair = psum_y.tile([P, O_BANKS, BANK], F32, tag="y")
+            everywhere = const.tile([P, O_BANKS, BANK], BF16, name="everywhere%d" % v)
+            for h in range(O_BANKS):
+                nc.tensor.matmul(
+                    bank_pair[:, h, :], lhsT=pick[:, v, :], rhs=vector_rows[:, h * BANK : (h + 1) * BANK], start=True, stop=True
+                )
+                nc.vector.tensor_copy(out=everywhere[:, h, :], in_=bank_pair[:, h, :])
+            spread.append(everywhere[:].rearrange("p h o -> p (h o)"))
+        bo_all, gamma_all, beta_all = spread
+
+        ksum_bank = psum_tp.tile([P, PACK, P], F32, tag="tp")
+        nc.tensor.transpose(ksum_bank[:, 0, :], ksum_rows[:].bitcast(F32), ident[:])
+        ksum = const.tile([P, B, PASSES, PACK], F32)
+        nc.vector.tensor_copy(
+            out=ksum[:].rearrange("p b g j -> p (b g j)"),
+            in_=ksum_bank[:, 0, 0:n_ksum_rows].bitcast(BF16),
+        )
+
+        q_grouped = keep.tile([P, B, PASSES, T, PACK], BF16, align_bytes=64)
+        q_codes = keep.tile([P, B, PASSES, T], U32, align_bytes=64)
+        q_scales = keep.tile([P, B, PASSES, T], U8, align_bytes=64)
+        kv_codes = keep.tile([P, B, PASSES, D], U32, align_bytes=64)
+        kv_scales = keep.tile([P, B, PASSES, D], U8, align_bytes=64)
+        wo_grouped = keep.tile([P, PASSES, D, PACK], BF16, align_bytes=64)
+        wo_codes = keep.tile([P, PASSES, D], U32, align_bytes=64)
+        wo_scales = keep.tile([P, PASSES, D], U8, align_bytes=64)
+        attn_codes = keep.tile([P, B, T_BLOCKS, PASSES, P], U32, align_bytes=64)
+        attn_scales = keep.tile([P, B, T_BLOCKS, PASSES, P], U8, align_bytes=64)
+
+        def transpose_rows(src_rows, dst_words):
+            bank = psum_tp.tile([P, PACK, P], F32, tag="tp")
+            for w in range(PASSES * HALVES):
+                nc.tensor.transpose(bank[:, w, :], src_rows.bitcast(F32)[:, w * P : (w + 1) * P], ident[:])
+            nc.scalar.copy(out=dst_words, in_=bank[:].rearrange("p (g u) r -> p g r u", g=PASSES))
+
+        def transpose_q(b, n):
+            transpose_rows(q_raw[b][:, n, :], q_grouped[:].bitcast(F32)[:, b, :, n * P : (n + 1) * P, :])
+
+        def transpose_wo(n):
+            transpose_rows(wo_raw[:, n, :], wo_grouped[:].bitcast(F32)[:, :, n * P : (n + 1) * P, :])
+
+        def quantise_q(b):
+            nc.vector.quantize_mx(
+                out=q_codes[:, b].rearrange("p g t -> p (g t)").bitcast(FP8X4),
+                scales=q_scales[:, b].rearrange("p g t -> p (g t)"),
+                in_=q_grouped[:, b].rearrange("p g t j -> p (g t j)"),
+            )
+
+        def quantise_wo(g):
+            nc.vector.quantize_mx(
+                out=wo_codes[:, g, :].bitcast(FP8X4),
+                scales=wo_scales[:, g, :],
+                in_=wo_grouped[:, g].rearrange("p o j -> p (o j)"),
+            )
+
+        def regroup_kv(kv_rows, copy):
+            kv_grouped = grouped.tile([P, PAIR, D // PAIR, PACK], BF16, align_bytes=64)
+            copy(out=kv_grouped[:], in_=kv_rows[:].rearrange("p j (c e) -> p e c j", e=PAIR))
+            return kv_grouped
+
+        def quantise_kv(b, g, kv_grouped):
+            nc.vector.quantize_mx(
+                out=kv_codes[:, b, g, :].bitcast(FP8X4),
+                scales=kv_scales[:, b, g, :],
+                in_=kv_grouped[:].rearrange("p e c j -> p (e c j)"),
+            )
+
+        def reciprocals(b, g, u, recip):
+            for j in range(u * PAIR, (u + 1) * PAIR):
+                nc.scalar.activation(
+                    out=recip[:, j, :],
+                    in_=q_grouped[:, b, g, :, j],
+                    func=ACT.Abs_reciprocal_sqrt,
+                    scale=ksum[:, b, g, j : j + 1],
+                    bias=eps_denom[:, 0:1],
+                )
+            quarter = recip[:, u * PAIR : (u + 1) * PAIR, :]
+            nc.scalar.activation(out=quarter, in_=quarter, func=ACT.Square)
+
+        def attention_products(b, n, recip):
+            tokens = slice(n * P, (n + 1) * P)
+            attn_grouped = stage.tile([P, PASSES, P, PACK], BF16, align_bytes=64)
+            for g_out in range(PASSES):
+                num = psum_num.tile([P, PACK, P], F32)
+                for j in range(PACK):
+                    u, e = divmod(j, PAIR)
+                    first = e * (D // PAIR) + (g_out * HALVES + u) * P
+                    features = slice(first, first + P)
+                    for g in range(PASSES):
+                        nc.tensor.matmul_mx(
+                            out=num[:, j, :],
+                            lhsT=kv_codes[:, b, g, features].bitcast(FP8X4),
+                            lhsT_scale=kv_scales[:, b, g, features],
+                            rhs=q_codes[:, b, g, tokens].bitcast(FP8X4),
+                            rhs_scale=q_scales[:, b, g, tokens],
+                            start=(g == 0),
+                            stop=(g == PASSES - 1),
+                        )
+                nc.vector.tensor_tensor(
+                    out=attn_grouped[:, g_out],
+                    in0=num[:].rearrange("p j t -> p t j"),
+                    in1=recip[g_out][:, :, tokens].rearrange("p j t -> p t j"),
+                    op=ALU.mult,
+                )
+            return attn_grouped
+
+        def quantise_attention(b, n, attn_grouped):
+            nc.vector.quantize_mx(
+                out=attn_codes[:, b, n].rearrange("p g t -> p (g t)").bitcast(FP8X4),
+                scales=attn_scales[:, b, n].rearrange("p g t -> p (g t)"),
+                in_=attn_grouped[:].rearrange("p g t j -> p (g t j)"),
+            )
+
+        def residual(b, n):
+            x = rows.tile([P, D], F32)
+            nc.vector.tensor_tensor(out=x[:], in0=audio_raw[b][:, n, :], in1=bo_all, op=ALU.add)
+            return x
+
+        def project(b, n, x):
+            y = psum_y.tile([P, O_BANKS, BANK], F32, tag="y")
+            sums = small.tile([P, O_BANKS], F32)
+            for h in range(O_BANKS):
+                outputs = slice(h * BANK, (h + 1) * BANK)
+                for g in range(PASSES):
+                    nc.tensor.matmul_mx(
+                        out=y[:, h, :],
+                        lhsT=attn_codes[:, b, n, g, :].bitcast(FP8X4),
+                        lhsT_scale=attn_scales[:, b, n, g, :],
+                        rhs=wo_codes[:, g, outputs].bitcast(FP8X4),
+                        rhs_scale=wo_scales[:, g, outputs],
+                        start=(g == 0),
+                        stop=(g == PASSES - 1),
+                    )
+            for h in range(O_BANKS):
+                outputs = slice(h * BANK, (h + 1) * BANK)
+                nc.vector.scalar_tensor_tensor(
+                    out=x[:, outputs],
+                    in0=y[:, h, :],
+                    scalar=1.0,
+                    in1=x[:, outputs],
+                    op0=ALU.mult,
+                    op1=ALU.add,
+                    accum_out=sums[:, h : h + 1],
+                )
+            neg_mean = small.tile([P, 1], F32)
+            nc.vector.tensor_scalar(
+                out=neg_mean[:], in0=sums[:, 0:1], scalar1=sums[:, 1:2], scalar2=-1.0 / D, op0=ALU.add, op1=ALU.mult
+            )
+            return neg_mean
+
+        def inverse_deviation(x, neg_mean):
+            squares = stage.tile([P, D], BF16)
+            sum_squares = small.tile([P, 1], F32)
+            nc.scalar.activation(
+                out=squares[:], in_=x[:], func=ACT.Square, bias=neg_mean[:, 0:1], accum_out=sum_squares[:, 0:1]
+            )
+            rstd = small.tile([P, 1], F32)
+            nc.scalar.activation(
+                out=rstd[:], in_=sum_squares[:], func=ACT.Abs_reciprocal_sqrt, scale=1.0 / D, bias=eps_ln[:, 0:1]
+            )
+            return rstd
+
+        def normalise_and_store(b, n, x, neg_mean, rstd):
+            nc.vector.scalar_tensor_tensor(
+                out=x[:], in0=x[:], scalar=neg_mean[:, 0:1], in1=gamma_all, op0=ALU.add, op1=ALU.mult
+            )
+            nc.vector.scalar_tensor_tensor(
+                out=x[:], in0=x[:], scalar=rstd[:, 0:1], in1=beta_all, op0=ALU.mult, op1=ALU.add
+            )
+            nc.sync.dma_start(out=out[b, n * P : (n + 1) * P, :], in_=x[:])
+
+        for n in range(T_BLOCKS):
+            transpose_q(0, n)
+        kv_grouped0 = regroup_kv(kv_raw[0], nc.vector.tensor_copy)
+        kv_raw.append(load_kv(1, 1))
+        nc.sync.dma_start(out=wo_raw[:], in_=Wo.rearrange("(n p) d -> p n d", p=P))
+        q_raw.append(load_tokens(q_feat[1]))
+        audio_raw = [load_tokens(audio[0]), load_tokens(audio[1])]
+        quantise_q(0)
+        kv_grouped1 = regroup_kv(kv_raw[1], nc.vector.tensor_copy)
+        quantise_kv(0, 0, kv_grouped0)
+        quantise_kv(0, 1, kv_grouped1)
+        recip0 = [recips.tile([P, PACK, T], F32, name="recip") for g in range(PASSES)]
+        for g in range(PASSES):
+            for u in range(HALVES):
+                reciprocals(0, g, u, recip0[g])
+
+        kv_grouped = []
+        attn_blocks = []
+        for n in range(T_BLOCKS):
+            if n < PASSES:
+                kv_grouped.append(regroup_kv(kv_raw[PASSES + n], nc.vector.tensor_copy))
+            else:
+                quantise_kv(1, n - PASSES, kv_grouped[n - PASSES])
+            attn_blocks.append(attention_products(0, n, recip0))
+            if n > 0:
+                quantise_attention(0, n - 1, attn_blocks[n - 1])
+            transpose_wo(2 * n)
+            transpose_wo(2 * n + 1)
+        quantise_attention(0, T_BLOCKS - 1, attn_blocks[T_BLOCKS - 1])
+        for n in range(T_BLOCKS):
+            transpose_q(1, n)
+        quantise_wo(0)
+        quantise_wo(1)
+        x = [residual(0, n) for n in range(AHEAD)]
+        quantise_q(1)
+
+        recip1 = [recips.tile([P, PACK, T], F32, name="recip") for g in range(PASSES)]
+        stats = []
+        for n in range(T_BLOCKS):
+            neg_mean = project(0, n, x[n])
+            reciprocals(1, n // HALVES, n % HALVES, recip1[n // HALVES])
+            stats.append((neg_mean, inverse_deviation(x[n], neg_mean)))
+            if n > 0:
+                normalise_and_store(0, n - 1, x[n - 1], stats[n - 1][0], stats[n - 1][1])
+            x.append(residual((n + AHEAD) // T_BLOCKS, (n + AHEAD) % T_BLOCKS))
+        last = T_BLOCKS - 1
+        normalise_and_store(0, last, x[last], stats[last][0], stats[last][1])
+
+        for s in range(T_BLOCKS + 2):
+            if s < T_BLOCKS:
+                attn_block = attention_products(1, s, recip1)
+            if 1 <= s <= T_BLOCKS:
+                i = T_BLOCKS + s - 1
+                neg_mean = project(1, s - 1, x[i])
+                stats.append((neg_mean, inverse_deviation(x[i], neg_mean)))
+                if s - 1 + AHEAD < T_BLOCKS:
+                    x.append(residual(1, s - 1 + AHEAD))
+            if s < T_BLOCKS:
+                quantise_attention(1, s, attn_block)
+            if s >= 2:
+                i = T_BLOCKS + s - 2
+                normalise_and_store(1, s - 2, x[i], stats[i][0], stats[i][1])

@@ -199,7 +199,7 @@ def tile_linearattentionlayer_pb_kernel(tc, q_feat, kv, k_sum, audio, Wo, bo, ga
 
         def residual(b, n):
             x = rows.tile([P, D], F32)
-            nc.vector.tensor_tensor(out=x[:], in0=audio_raw[b][:, n, :], in1=bo_all, op=ALU.add)
+            nc.gpsimd.tensor_tensor(out=x[:], in0=audio_raw[b][:, n, :], in1=bo_all, op=ALU.add)
             return x
 
         def project(b, n, x):

@@ -24,7 +24,9 @@ T_BLOCKS = T // P
 ROW_BLOCKS = D // P
 BANK = 512
 O_BANKS = D // BANK
+N_BLOCKS = B * T_BLOCKS
 AHEAD = 2
+FIRST = T_BLOCKS - 1
 FLOPS = 2 * (2 * B * T * D * D)
 
 
@@ -37,11 +39,11 @@ def tile_linearattentionlayer_pb_kernel(tc, q_feat, kv, k_sum, audio, Wo, bo, ga
         grouped = stack.enter_context(tc.tile_pool(name="grouped", bufs=2))
         recips = stack.enter_context(tc.tile_pool(name="recips", bufs=3))
         stage = stack.enter_context(tc.tile_pool(name="stage", bufs=2))
-        rows = stack.enter_context(tc.tile_pool(name="rows", bufs=6))
+        rows = stack.enter_context(tc.tile_pool(name="rows", bufs=7))
         small = stack.enter_context(tc.tile_pool(name="small", bufs=4))
-        psum_tp = stack.enter_context(tc.psum_pool(name="psum_tp", bufs=2))
-        psum_num = stack.enter_context(tc.psum_pool(name="psum_num", bufs=2))
+        psum_const = stack.enter_context(tc.psum_pool(name="psum_const", bufs=1))
         psum_y = stack.enter_context(tc.psum_pool(name="psum_y", bufs=2))
+        psum_bank = stack.enter_context(tc.psum_pool(name="psum_bank", bufs=4))
         stack.enter_context(tc.manual_schedule())
 
         ident = const.tile([P, P], F32)
@@ -82,19 +84,21 @@ def tile_linearattentionlayer_pb_kernel(tc, q_feat, kv, k_sum, audio, Wo, bo, ga
         q_raw = [load_tokens(q_feat[0])]
         kv_raw = [load_kv(0, 0), load_kv(0, 1), load_kv(1, 0)]
 
-        spread = []
-        for v in range(len(vectors)):
-            bank_pair = psum_y.tile([P, O_BANKS, BANK], F32, tag="y")
-            everywhere = const.tile([P, O_BANKS, BANK], BF16, name="everywhere%d" % v)
+        def spread(v, bank):
             for h in range(O_BANKS):
-                nc.tensor.matmul(
-                    bank_pair[:, h, :], lhsT=pick[:, v, :], rhs=vector_rows[:, h * BANK : (h + 1) * BANK], start=True, stop=True
-                )
-                nc.vector.tensor_copy(out=everywhere[:, h, :], in_=bank_pair[:, h, :])
-            spread.append(everywhere[:].rearrange("p h o -> p (h o)"))
-        bo_all, gamma_all, beta_all = spread
+                outputs = slice(h * BANK, (h + 1) * BANK)
+                nc.tensor.matmul(bank[:, outputs], lhsT=pick[:, v, :], rhs=vector_rows[:, outputs], start=True, stop=True)
 
-        ksum_bank = psum_tp.tile([P, PACK, P], F32, tag="tp")
+        bo_bank = psum_y.tile([P, D], BF16, tag="y")
+        spread(0, bo_bank)
+        bo_all = const.tile([P, D], BF16)
+        nc.vector.tensor_copy(out=bo_all[:], in_=bo_bank[:])
+        gamma_all = psum_const.tile([P, D], BF16)
+        spread(1, gamma_all)
+        beta_all = psum_const.tile([P, D], BF16)
+        spread(2, beta_all)
+
+        ksum_bank = psum_bank.tile([P, PACK, P], F32, tag="bank")
         nc.tensor.transpose(ksum_bank[:, 0, :], ksum_rows[:].bitcast(F32), ident[:])
         ksum = const.tile([P, B, PASSES, PACK], F32)
         nc.vector.tensor_copy(
@@ -114,7 +118,7 @@ def tile_linearattentionlayer_pb_kernel(tc, q_feat, kv, k_sum, audio, Wo, bo, ga
         attn_scales = keep.tile([P, B, T_BLOCKS, PASSES, P], U8, align_bytes=64)
 
         def transpose_rows(src_rows, dst_words):
-            bank = psum_tp.tile([P, PACK, P], F32, tag="tp")
+            bank = psum_bank.tile([P, PACK, P], F32, tag="bank")
             for w in range(PASSES * HALVES):
                 nc.tensor.transpose(bank[:, w, :], src_rows.bitcast(F32)[:, w * P : (w + 1) * P], ident[:])
             nc.scalar.copy(out=dst_words, in_=bank[:].rearrange("p (g u) r -> p g r u", g=PASSES))
@@ -167,7 +171,7 @@ def tile_linearattentionlayer_pb_kernel(tc, q_feat, kv, k_sum, audio, Wo, bo, ga
             tokens = slice(n * P, (n + 1) * P)
             attn_grouped = stage.tile([P, PASSES, P, PACK], BF16, align_bytes=64)
             for g_out in range(PASSES):
-                num = psum_num.tile([P, PACK, P], F32)
+                num = psum_bank.tile([P, PACK, P], F32, tag="bank")
                 for j in range(PACK):
                     u, e = divmod(j, PAIR)
                     first = e * (D // PAIR) + (g_out * HALVES + u) * P
@@ -197,19 +201,21 @@ def tile_linearattentionlayer_pb_kernel(tc, q_feat, kv, k_sum, audio, Wo, bo, ga
                 in_=attn_grouped[:].rearrange("p g t j -> p (g t j)"),
             )
 
-        def residual(b, n):
+        def residual(i):
+            b, n = divmod(i, T_BLOCKS)
             x = rows.tile([P, D], F32)
-            nc.gpsimd.tensor_tensor(out=x[:], in0=audio_raw[b][:, n, :], in1=bo_all, op=ALU.add)
+            nc.gpsimd.tensor_tensor(out=x[:], in0=audio_raw[b][:, n, :], in1=bo_all[:], op=ALU.add)
             return x
 
-        def project(b, n, x):
-            y = psum_y.tile([P, O_BANKS, BANK], F32, tag="y")
+        def project(i, x):
+            b, n = divmod(i, T_BLOCKS)
+            y = [psum_y.tile([P, BANK], F32, name="y") for h in range(O_BANKS)]
             sums = small.tile([P, O_BANKS], F32)
             for h in range(O_BANKS):
                 outputs = slice(h * BANK, (h + 1) * BANK)
                 for g in range(PASSES):
                     nc.tensor.matmul_mx(
-                        out=y[:, h, :],
+                        out=y[h][:],
                         lhsT=attn_codes[:, b, n, g, :].bitcast(FP8X4),
                         lhsT_scale=attn_scales[:, b, n, g, :],
                         rhs=wo_codes[:, g, outputs].bitcast(FP8X4),
@@ -221,20 +227,18 @@ def tile_linearattentionlayer_pb_kernel(tc, q_feat, kv, k_sum, audio, Wo, bo, ga
                 outputs = slice(h * BANK, (h + 1) * BANK)
                 nc.vector.scalar_tensor_tensor(
                     out=x[:, outputs],
-                    in0=y[:, h, :],
+                    in0=y[h][:],
                     scalar=1.0,
                     in1=x[:, outputs],
                     op0=ALU.mult,
                     op1=ALU.add,
                     accum_out=sums[:, h : h + 1],
                 )
+            scaled_sums = small.tile([P, O_BANKS], F32)
             neg_mean = small.tile([P, 1], F32)
-            nc.vector.tensor_scalar(
-                out=neg_mean[:], in0=sums[:, 0:1], scalar1=sums[:, 1:2], scalar2=-1.0 / D, op0=ALU.add, op1=ALU.mult
+            nc.scalar.activation(
+                out=scaled_sums[:], in_=sums[:], func=ACT.Identity, scale=-1.0 / D, accum_out=neg_mean[:, 0:1]
             )
-            return neg_mean
-
-        def inverse_deviation(x, neg_mean):
             squares = stage.tile([P, D], BF16)
             sum_squares = small.tile([P, 1], F32)
             nc.scalar.activation(
@@ -244,14 +248,17 @@ def tile_linearattentionlayer_pb_kernel(tc, q_feat, kv, k_sum, audio, Wo, bo, ga
             nc.scalar.activation(
                 out=rstd[:], in_=sum_squares[:], func=ACT.Abs_reciprocal_sqrt, scale=1.0 / D, bias=eps_ln[:, 0:1]
             )
-            return rstd
+            return neg_mean, rstd
 
-        def normalise_and_store(b, n, x, neg_mean, rstd):
+        def centre_and_scale(x, neg_mean):
             nc.vector.scalar_tensor_tensor(
-                out=x[:], in0=x[:], scalar=neg_mean[:, 0:1], in1=gamma_all, op0=ALU.add, op1=ALU.mult
+                out=x[:], in0=x[:], scalar=neg_mean[:, 0:1], in1=gamma_all[:], op0=ALU.add, op1=ALU.mult
             )
+
+        def shift_and_store(i, x, rstd):
+            b, n = divmod(i, T_BLOCKS)
             nc.vector.scalar_tensor_tensor(
-                out=x[:], in0=x[:], scalar=rstd[:, 0:1], in1=beta_all, op0=ALU.mult, op1=ALU.add
+                out=x[:], in0=x[:], scalar=rstd[:, 0:1], in1=beta_all[:], op0=ALU.mult, op1=ALU.add
             )
             nc.sync.dma_start(out=out[b, n * P : (n + 1) * P, :], in_=x[:])
 
@@ -259,12 +266,12 @@ def tile_linearattentionlayer_pb_kernel(tc, q_feat, kv, k_sum, audio, Wo, bo, ga
             transpose_q(0, n)
         kv_grouped0 = regroup_kv(kv_raw[0], nc.vector.tensor_copy)
         kv_raw.append(load_kv(1, 1))
-        nc.sync.dma_start(out=wo_raw[:], in_=Wo.rearrange("(n p) d -> p n d", p=P))
         q_raw.append(load_tokens(q_feat[1]))
+        nc.sync.dma_start(out=wo_raw[:], in_=Wo.rearrange("(n p) d -> p n d", p=P))
         audio_raw = [load_tokens(audio[0]), load_tokens(audio[1])]
-        quantise_q(0)
         kv_grouped1 = regroup_kv(kv_raw[1], nc.vector.tensor_copy)
         quantise_kv(0, 0, kv_grouped0)
+        quantise_q(0)
         quantise_kv(0, 1, kv_grouped1)
         recip0 = [recips.tile([P, PACK, T], F32, name="recip") for g in range(PASSES)]
         for g in range(PASSES):
@@ -281,39 +288,30 @@ def tile_linearattentionlayer_pb_kernel(tc, q_feat, kv, k_sum, audio, Wo, bo, ga
             attn_blocks.append(attention_products(0, n, recip0))
             if n > 0:
                 quantise_attention(0, n - 1, attn_blocks[n - 1])
+            transpose_q(1, n)
             transpose_wo(2 * n)
             transpose_wo(2 * n + 1)
         quantise_attention(0, T_BLOCKS - 1, attn_blocks[T_BLOCKS - 1])
-        for n in range(T_BLOCKS):
-            transpose_q(1, n)
         quantise_wo(0)
         quantise_wo(1)
-        x = [residual(0, n) for n in range(AHEAD)]
+        x = [residual(i) for i in range(AHEAD)]
         quantise_q(1)
 
         recip1 = [recips.tile([P, PACK, T], F32, name="recip") for g in range(PASSES)]
+        reciprocals(1, 0, 0, recip1[0])
         stats = []
-        for n in range(T_BLOCKS):
-            neg_mean = project(0, n, x[n])
-            reciprocals(1, n // HALVES, n % HALVES, recip1[n // HALVES])
-            stats.append((neg_mean, inverse_deviation(x[n], neg_mean)))
-            if n > 0:
-                normalise_and_store(0, n - 1, x[n - 1], stats[n - 1][0], stats[n - 1][1])
-            x.append(residual((n + AHEAD) // T_BLOCKS, (n + AHEAD) % T_BLOCKS))
-        last = T_BLOCKS - 1
-        normalise_and_store(0, last, x[last], stats[last][0], stats[last][1])
-
-        for s in range(T_BLOCKS + 2):
-            if s < T_BLOCKS:
-                attn_block = attention_products(1, s, recip1)
-            if 1 <= s <= T_BLOCKS:
-                i = T_BLOCKS + s - 1
-                neg_mean = project(1, s - 1, x[i])
-                stats.append((neg_mean, inverse_deviation(x[i], neg_mean)))
-                if s - 1 + AHEAD < T_BLOCKS:
-                    x.append(residual(1, s - 1 + AHEAD))
-            if s < T_BLOCKS:
-                quantise_attention(1, s, attn_block)
+        for s in range(N_BLOCKS + 2):
+            if s + 1 < PASSES * HALVES:
+                reciprocals(1, (s + 1) // HALVES, (s + 1) % HALVES, recip1[(s + 1) // HALVES])
+            if s < N_BLOCKS:
+                stats.append(project(s, x[s]))
+            if FIRST <= s < FIRST + T_BLOCKS:
+                attn_block = attention_products(1, s - FIRST, recip1)
             if s >= 2:
-                i = T_BLOCKS + s - 2
-                normalise_and_store(1, s - 2, x[i], stats[i][0], stats[i][1])
+                shift_and_store(s - 2, x[s - 2], stats[s - 2][1])
+            if FIRST <= s < FIRST + T_BLOCKS:
+                quantise_attention(1, s - FIRST, attn_block)
+            if 1 <= s <= N_BLOCKS:
+                centre_and_scale(x[s - 1], stats[s - 1][0])
+            if s + AHEAD < N_BLOCKS:
+                x.append(residual(s + AHEAD))

@@ -63,9 +63,9 @@ def tile_linearattentionlayer_pb_kernel(tc, q_feat, kv, k_sum, audio, Wo, bo, ga
             nc.vector.memset(pick[32 * v : 32 * v + 1, v, :], 1.0)
 
         n_ksum_rows = B * D // (PAIR * P)
-        nc.sync.dma_start(out=ksum_rows[0:n_ksum_rows, :], in_=k_sum.rearrange("b (r c) -> (b r) c", c=PAIR * P))
+        nc.scalar.dma_start(out=ksum_rows[0:n_ksum_rows, :], in_=k_sum.rearrange("b (r c) -> (b r) c", c=PAIR * P))
         for v in range(len(vectors)):
-            nc.sync.dma_start(out=vector_rows[32 * v : 32 * v + 1, :], in_=vectors[v].unsqueeze(0))
+            nc.scalar.dma_start(out=vector_rows[32 * v : 32 * v + 1, :], in_=vectors[v].unsqueeze(0))
         wo_raw = const.tile([P, ROW_BLOCKS, D], BF16)
 
         def load_tokens(src):
@@ -145,7 +145,10 @@ def tile_linearattentionlayer_pb_kernel(tc, q_feat, kv, k_sum, audio, Wo, bo, ga
 
         def regroup_kv(kv_rows, copy):
             kv_grouped = grouped.tile([P, PAIR, D // PAIR, PACK], BF16, align_bytes=64)
-            copy(out=kv_grouped[:], in_=kv_rows[:].rearrange("p j (c e) -> p e c j", e=PAIR))
+            copy(
+                out=kv_grouped[:].rearrange("p e c j -> p c j e"),
+                in_=kv_rows[:].rearrange("p j (c e) -> p c j e", e=PAIR),
+            )
             return kv_grouped
 
         def quantise_kv(b, g, kv_grouped):

@@ -39,7 +39,7 @@ def tile_linearattentionlayer_pb_kernel(tc, q_feat, kv, k_sum, audio, Wo, bo, ga
         grouped = stack.enter_context(tc.tile_pool(name="grouped", bufs=2))
         recips = stack.enter_context(tc.tile_pool(name="recips", bufs=3))
         stage = stack.enter_context(tc.tile_pool(name="stage", bufs=2))
-        rows = stack.enter_context(tc.tile_pool(name="rows", bufs=7))
+        rows = stack.enter_context(tc.tile_pool(name="rows", bufs=8))
         small = stack.enter_context(tc.tile_pool(name="small", bufs=4))
         psum_const = stack.enter_context(tc.psum_pool(name="psum_const", bufs=1))
         psum_y = stack.enter_context(tc.psum_pool(name="psum_y", bufs=2))
@@ -63,9 +63,6 @@ def tile_linearattentionlayer_pb_kernel(tc, q_feat, kv, k_sum, audio, Wo, bo, ga
             nc.vector.memset(pick[32 * v : 32 * v + 1, v, :], 1.0)
 
         n_ksum_rows = B * D // (PAIR * P)
-        nc.scalar.dma_start(out=ksum_rows[0:n_ksum_rows, :], in_=k_sum.rearrange("b (r c) -> (b r) c", c=PAIR * P))
-        for v in range(len(vectors)):
-            nc.scalar.dma_start(out=vector_rows[32 * v : 32 * v + 1, :], in_=vectors[v].unsqueeze(0))
         wo_raw = const.tile([P, ROW_BLOCKS, D], BF16)
 
         def load_tokens(src):
@@ -82,29 +79,10 @@ def tile_linearattentionlayer_pb_kernel(tc, q_feat, kv, k_sum, audio, Wo, bo, ga
             return kv_rows
 
         q_raw = [load_tokens(q_feat[0])]
+        nc.sync.dma_start(out=ksum_rows[0:n_ksum_rows, :], in_=k_sum.rearrange("b (r c) -> (b r) c", c=PAIR * P))
         kv_raw = [load_kv(0, 0), load_kv(0, 1), load_kv(1, 0)]
-
-        def spread(v, bank):
-            for h in range(O_BANKS):
-                outputs = slice(h * BANK, (h + 1) * BANK)
-                nc.tensor.matmul(bank[:, outputs], lhsT=pick[:, v, :], rhs=vector_rows[:, outputs], start=True, stop=True)
-
-        bo_bank = psum_y.tile([P, D], BF16, tag="y")
-        spread(0, bo_bank)
-        bo_all = const.tile([P, D], BF16)
-        nc.vector.tensor_copy(out=bo_all[:], in_=bo_bank[:])
-        gamma_all = psum_const.tile([P, D], BF16)
-        spread(1, gamma_all)
-        beta_all = psum_const.tile([P, D], BF16)
-        spread(2, beta_all)
-
-        ksum_bank = psum_bank.tile([P, PACK, P], F32, tag="bank")
-        nc.tensor.transpose(ksum_bank[:, 0, :], ksum_rows[:].bitcast(F32), ident[:])
-        ksum = const.tile([P, B, PASSES, PACK], F32)
-        nc.vector.tensor_copy(
-            out=ksum[:].rearrange("p b g j -> p (b g j)"),
-            in_=ksum_bank[:, 0, 0:n_ksum_rows].bitcast(BF16),
-        )
+        for v in range(len(vectors)):
+            nc.sync.dma_start(out=vector_rows[32 * v : 32 * v + 1, :], in_=vectors[v].unsqueeze(0))
 
         q_grouped = keep.tile([P, B, PASSES, T, PACK], BF16, align_bytes=64)
         q_codes = keep.tile([P, B, PASSES, T], U32, align_bytes=64)
@@ -145,10 +123,7 @@ def tile_linearattentionlayer_pb_kernel(tc, q_feat, kv, k_sum, audio, Wo, bo, ga
 
         def regroup_kv(kv_rows, copy):
             kv_grouped = grouped.tile([P, PAIR, D // PAIR, PACK], BF16, align_bytes=64)
-            copy(
-                out=kv_grouped[:].rearrange("p e c j -> p c j e"),
-                in_=kv_rows[:].rearrange("p j (c e) -> p c j e", e=PAIR),
-            )
+            copy(out=kv_grouped[:], in_=kv_rows[:].rearrange("p j (c e) -> p e c j", e=PAIR))
             return kv_grouped
 
         def quantise_kv(b, g, kv_grouped):
@@ -260,13 +235,41 @@ def tile_linearattentionlayer_pb_kernel(tc, q_feat, kv, k_sum, audio, Wo, bo, ga
 
         def shift_and_store(i, x, rstd):
             b, n = divmod(i, T_BLOCKS)
-            nc.vector.scalar_tensor_tensor(
-                out=x[:], in0=x[:], scalar=rstd[:, 0:1], in1=beta_all[:], op0=ALU.mult, op1=ALU.add
-            )
-            nc.sync.dma_start(out=out[b, n * P : (n + 1) * P, :], in_=x[:])
+            if 1 <= i < N_BLOCKS - 3:
+                nc.scalar.activation(out=x[:], in_=x[:], func=ACT.Copy, scale=rstd[:, 0:1])
+                nc.gpsimd.tensor_tensor(out=x[:], in0=x[:], in1=beta_sbuf[:], op=ALU.add)
+                nc.gpsimd.dma_start(out=out[b, n * P : (n + 1) * P, :], in_=x[:])
+            else:
+                nc.vector.scalar_tensor_tensor(
+                    out=x[:], in0=x[:], scalar=rstd[:, 0:1], in1=beta_all[:], op0=ALU.mult, op1=ALU.add
+                )
+                nc.sync.dma_start(out=out[b, n * P : (n + 1) * P, :], in_=x[:])
 
         for n in range(T_BLOCKS):
             transpose_q(0, n)
+
+        ksum_bank = psum_bank.tile([P, PACK, P], F32, tag="bank")
+        nc.tensor.transpose(ksum_bank[:, 0, :], ksum_rows[:].bitcast(F32), ident[:])
+        ksum = const.tile([P, B, PASSES, PACK], F32)
+        nc.scalar.copy(
+            out=ksum[:].rearrange("p b g j -> p (b g j)"),
+            in_=ksum_bank[:, 0, 0:n_ksum_rows].bitcast(BF16),
+        )
+
+        def spread(v, bank):
+            for h in range(O_BANKS):
+                outputs = slice(h * BANK, (h + 1) * BANK)
+                nc.tensor.matmul(bank[:, outputs], lhsT=pick[:, v, :], rhs=vector_rows[:, outputs], start=True, stop=True)
+
+        bo_bank = psum_y.tile([P, D], BF16, tag="y")
+        spread(0, bo_bank)
+        bo_all = const.tile([P, D], BF16)
+        gamma_all = psum_const.tile([P, D], BF16)
+        spread(1, gamma_all)
+        beta_all = psum_const.tile([P, D], BF16)
+        spread(2, beta_all)
+        beta_sbuf = const.tile([P, D], BF16)
+
         kv_grouped0 = regroup_kv(kv_raw[0], nc.vector.tensor_copy)
         kv_raw.append(load_kv(1, 1))
         q_raw.append(load_tokens(q_feat[1]))
@@ -280,6 +283,8 @@ def tile_linearattentionlayer_pb_kernel(tc, q_feat, kv, k_sum, audio, Wo, bo, ga
         for g in range(PASSES):
             for u in range(HALVES):
                 reciprocals(0, g, u, recip0[g])
+        nc.scalar.copy(out=bo_all[:], in_=bo_bank[:])
+        nc.scalar.copy(out=beta_sbuf[:], in_=beta_all[:])
 
         kv_grouped = []
         attn_blocks = []
@@ -306,6 +311,8 @@ def tile_linearattentionlayer_pb_kernel(tc, q_feat, kv, k_sum, audio, Wo, bo, ga
         for s in range(N_BLOCKS + 2):
             if s + 1 < PASSES * HALVES:
                 reciprocals(1, (s + 1) // HALVES, (s + 1) % HALVES, recip1[(s + 1) // HALVES])
+            if s + AHEAD < N_BLOCKS:
+                x.append(residual(s + AHEAD))
             if s < N_BLOCKS:
                 stats.append(project(s, x[s]))
             if FIRST <= s < FIRST + T_BLOCKS:
@@ -316,5 +323,3 @@ def tile_linearattentionlayer_pb_kernel(tc, q_feat, kv, k_sum, audio, Wo, bo, ga
                 quantise_attention(1, s - FIRST, attn_block)
             if 1 <= s <= N_BLOCKS:
                 centre_and_scale(x[s - 1], stats[s - 1][0])
-            if s + AHEAD < N_BLOCKS:
-                x.append(residual(s + AHEAD))

@@ -238,7 +238,7 @@ def tile_linearattentionlayer_pb_kernel(tc, q_feat, kv, k_sum, audio, Wo, bo, ga
             if 1 <= i < N_BLOCKS - 3:
                 nc.scalar.activation(out=x[:], in_=x[:], func=ACT.Copy, scale=rstd[:, 0:1])
                 nc.gpsimd.tensor_tensor(out=x[:], in0=x[:], in1=beta_sbuf[:], op=ALU.add)
-                nc.gpsimd.dma_start(out=out[b, n * P : (n + 1) * P, :], in_=x[:])
+                nc.sync.dma_start(out=out[b, n * P : (n + 1) * P, :], in_=x[:])
             else:
                 nc.vector.scalar_tensor_tensor(
                     out=x[:], in0=x[:], scalar=rstd[:, 0:1], in1=beta_all[:], op0=ALU.mult, op1=ALU.add

@@ -21,12 +21,13 @@ HALVES = PACK // PAIR
 K_PASS = P * PACK
 PASSES = D // K_PASS
 T_BLOCKS = T // P
-ROW_BLOCKS = D // P
+CHUNKS = D // P
 BANK = 512
 O_BANKS = D // BANK
 N_BLOCKS = B * T_BLOCKS
-AHEAD = 2
-FIRST = T_BLOCKS - 1
+T_HALF = T // 2
+FIRST = T_BLOCKS - 2
+N_VEC = 2
 FLOPS = 2 * (2 * B * T * D * D)
 
 
@@ -37,52 +38,75 @@ def tile_linearattentionlayer_pb_kernel(tc, q_feat, kv, k_sum, audio, Wo, bo, ga
         raw = stack.enter_context(tc.tile_pool(name="raw", bufs=3))
         keep = stack.enter_context(tc.tile_pool(name="keep", bufs=1))
         grouped = stack.enter_context(tc.tile_pool(name="grouped", bufs=2))
-        recips = stack.enter_context(tc.tile_pool(name="recips", bufs=3))
+        recips = stack.enter_context(tc.tile_pool(name="recips", bufs=4))
         stage = stack.enter_context(tc.tile_pool(name="stage", bufs=2))
-        rows = stack.enter_context(tc.tile_pool(name="rows", bufs=8))
+        turned = stack.enter_context(tc.tile_pool(name="turned", bufs=3))
+        rows = stack.enter_context(tc.tile_pool(name="rows", bufs=5))
         small = stack.enter_context(tc.tile_pool(name="small", bufs=4))
-        psum_const = stack.enter_context(tc.psum_pool(name="psum_const", bufs=1))
-        psum_y = stack.enter_context(tc.psum_pool(name="psum_y", bufs=2))
         psum_bank = stack.enter_context(tc.psum_pool(name="psum_bank", bufs=4))
+        psum_x = stack.enter_context(tc.psum_pool(name="psum_x", bufs=4))
         stack.enter_context(tc.manual_schedule())
+
+        n_ksum_rows = B * D // (PAIR * P)
+        ksum_rows = const.tile([P, PAIR * P], BF16)
+        nc.vector.memset(ksum_rows[:], 0.0)
+        bo_rows = const.tile([P, P], BF16)
+        nc.vector.memset(bo_rows[:], 0.0)
+        wo_raw = const.tile([P, CHUNKS, D], BF16)
+        gamma_all = const.tile([P, D], BF16)
+        beta_all = const.tile([P, D], BF16)
+
+        def load_tokens(src, pieces):
+            token_rows = raw.tile([P, T_BLOCKS, D], BF16)
+            step = T_BLOCKS // pieces
+            for n in range(0, T_BLOCKS, step):
+                nc.sync.dma_start(
+                    out=token_rows[:, n : n + step, :],
+                    in_=src[n * P : (n + step) * P, :].rearrange("(n p) d -> p n d", p=P),
+                )
+            return token_rows
+
+        def load_kv(b, g, pieces):
+            kv_rows = raw.tile([P, PACK, D], BF16)
+            width = D // pieces
+            for i in range(pieces):
+                columns = slice(i * width, (i + 1) * width)
+                for u in range(HALVES) if pieces > 1 else range(1):
+                    rows_u = slice(g * K_PASS + u * PAIR * P, g * K_PASS + (u + 1) * PAIR * P)
+                    if pieces > 1:
+                        nc.sync.dma_start(
+                            out=kv_rows[:, u * PAIR : (u + 1) * PAIR, columns],
+                            in_=kv[b, rows_u, columns].rearrange("(p e) c -> p e c", p=P),
+                        )
+                    else:
+                        nc.sync.dma_start(
+                            out=kv_rows[:].rearrange("p (u e) c -> p u (e c)", u=HALVES),
+                            in_=kv[b, g * K_PASS : (g + 1) * K_PASS, :].rearrange("(u p e) c -> p u (e c)", u=HALVES, p=P),
+                        )
+            return kv_rows
+
+        kv_raw = [load_kv(0, 0, 2)]
+        kv_raw.append(load_kv(0, 1, 2))
+        q_raw = [load_tokens(q_feat[0], T_BLOCKS)]
+        nc.sync.dma_start(out=ksum_rows[0:n_ksum_rows, :], in_=k_sum.rearrange("b (r c) -> (b r) c", c=PAIR * P))
+        kv_raw.append(load_kv(1, 0, 2))
+        nc.sync.dma_start(out=bo_rows[0:CHUNKS, :], in_=bo.rearrange("(m p) -> m p", p=P))
+        for n in range(0, CHUNKS, CHUNKS // 2):
+            nc.sync.dma_start(
+                out=wo_raw[:, n : n + CHUNKS // 2, :],
+                in_=Wo[n * P : (n + CHUNKS // 2) * P, :].rearrange("(n p) d -> p n d", p=P),
+            )
+
+        q_raw.append(load_tokens(q_feat[1], 1))
 
         ident = const.tile([P, P], F32)
         make_identity(nc, ident[:])
+        ident_bf = const.tile([P, P], BF16)
+        make_identity(nc, ident_bf[:])
         eps_denom = const.tile([P, 1], F32)
         nc.vector.memset(eps_denom[:], EPS_DENOM)
         eps_ln = const.tile([P, 1], F32)
         nc.vector.memset(eps_ln[:], EPS_LN)
-        ksum_rows = const.tile([P, PAIR * P], BF16)
-        nc.vector.memset(ksum_rows[:], 0.0)
-        vectors = (bo, gamma, beta)
-        vector_rows = const.tile([P, D], BF16)
-        nc.vector.memset(vector_rows[:], 0.0)
-        pick = const.tile([P, len(vectors), P], BF16)
-        nc.vector.memset(pick[:], 0.0)
-        for v in range(len(vectors)):
-            nc.vector.memset(pick[32 * v : 32 * v + 1, v, :], 1.0)
-
-        n_ksum_rows = B * D // (PAIR * P)
-        wo_raw = const.tile([P, ROW_BLOCKS, D], BF16)
-
-        def load_tokens(src):
-            token_rows = raw.tile([P, T_BLOCKS, D], BF16)
-            nc.sync.dma_start(out=token_rows[:], in_=src.rearrange("(n p) d -> p n d", p=P))
-            return token_rows
-
-        def load_kv(b, g):
-            kv_rows = raw.tile([P, PACK, D], BF16)
-            nc.sync.dma_start(
-                out=kv_rows[:].rearrange("p (u e) c -> p u (e c)", u=HALVES),
-                in_=kv[b, g * K_PASS : (g + 1) * K_PASS, :].rearrange("(u p e) c -> p u (e c)", u=HALVES, p=P),
-            )
-            return kv_rows
-
-        q_raw = [load_tokens(q_feat[0])]
-        nc.sync.dma_start(out=ksum_rows[0:n_ksum_rows, :], in_=k_sum.rearrange("b (r c) -> (b r) c", c=PAIR * P))
-        kv_raw = [load_kv(0, 0), load_kv(0, 1), load_kv(1, 0)]
-        for v in range(len(vectors)):
-            nc.sync.dma_start(out=vector_rows[32 * v : 32 * v + 1, :], in_=vectors[v].unsqueeze(0))
 
         q_grouped = keep.tile([P, B, PASSES, T, PACK], BF16, align_bytes=64)
         q_codes = keep.tile([P, B, PASSES, T], U32, align_bytes=64)
@@ -96,7 +120,7 @@ def tile_linearattentionlayer_pb_kernel(tc, q_feat, kv, k_sum, audio, Wo, bo, ga
         attn_scales = keep.tile([P, B, T_BLOCKS, PASSES, P], U8, align_bytes=64)
 
         def transpose_rows(src_rows, dst_words):
-            bank = psum_bank.tile([P, PACK, P], F32, tag="bank")
+            bank = psum_x.tile([P, PACK, P], F32, tag="x")
             for w in range(PASSES * HALVES):
                 nc.tensor.transpose(bank[:, w, :], src_rows.bitcast(F32)[:, w * P : (w + 1) * P], ident[:])
             nc.scalar.copy(out=dst_words, in_=bank[:].rearrange("p (g u) r -> p g r u", g=PASSES))
@@ -121,9 +145,15 @@ def tile_linearattentionlayer_pb_kernel(tc, q_feat, kv, k_sum, audio, Wo, bo, ga
                 in_=wo_grouped[:, g].rearrange("p o j -> p (o j)"),
             )
 
-        def regroup_kv(kv_rows, copy):
+        def regroup_kv(kv_rows, pieces, on_scalar=()):
             kv_grouped = grouped.tile([P, PAIR, D // PAIR, PACK], BF16, align_bytes=64)
-            copy(out=kv_grouped[:], in_=kv_rows[:].rearrange("p j (c e) -> p e c j", e=PAIR))
+            width = D // pieces
+            for i in range(pieces):
+                copy = nc.scalar.copy if i in on_scalar else nc.vector.tensor_copy
+                copy(
+                    out=kv_grouped[:, :, i * width // PAIR : (i + 1) * width // PAIR, :],
+                    in_=kv_rows[:, :, i * width : (i + 1) * width].rearrange("p j (c e) -> p e c j", e=PAIR),
+                )
             return kv_grouped
 
         def quantise_kv(b, g, kv_grouped):
@@ -133,17 +163,17 @@ def tile_linearattentionlayer_pb_kernel(tc, q_feat, kv, k_sum, audio, Wo, bo, ga
                 in_=kv_grouped[:].rearrange("p e c j -> p (e c j)"),
             )
 
-        def reciprocals(b, g, u, recip):
-            for j in range(u * PAIR, (u + 1) * PAIR):
+        def reciprocals(b, h, g, recip):
+            tokens = slice(h * T_HALF, (h + 1) * T_HALF)
+            for j in range(PACK):
                 nc.scalar.activation(
-                    out=recip[:, j, :],
-                    in_=q_grouped[:, b, g, :, j],
+                    out=recip[:, j, tokens],
+                    in_=q_grouped[:, b, g, tokens, j],
                     func=ACT.Abs_reciprocal_sqrt,
                     scale=ksum[:, b, g, j : j + 1],
                     bias=eps_denom[:, 0:1],
                 )
-            quarter = recip[:, u * PAIR : (u + 1) * PAIR, :]
-            nc.scalar.activation(out=quarter, in_=quarter, func=ACT.Square)
+            nc.scalar.activation(out=recip[:, :, tokens], in_=recip[:, :, tokens], func=ACT.Square)
 
         def attention_products(b, n, recip):
             tokens = slice(n * P, (n + 1) * P)
@@ -179,71 +209,97 @@ def tile_linearattentionlayer_pb_kernel(tc, q_feat, kv, k_sum, audio, Wo, bo, ga
                 in_=attn_grouped[:].rearrange("p g t j -> p (g t j)"),
             )
 
-        def residual(i):
+        def project(i):
             b, n = divmod(i, T_BLOCKS)
-            x = rows.tile([P, D], F32)
-            nc.gpsimd.tensor_tensor(out=x[:], in0=audio_raw[b][:, n, :], in1=bo_all[:], op=ALU.add)
+            y_turned = turned.tile([P, CHUNKS, P], F32)
+            for h in range(O_BANKS):
+                bank = psum_bank.tile([P, PACK, P], F32, tag="bank")
+                for k in range(PACK):
+                    m = h * PACK + k
+                    outputs = slice(m * P, (m + 1) * P)
+                    for g in range(PASSES):
+                        nc.tensor.matmul_mx(
+                            out=bank[:, k, :],
+                            lhsT=wo_codes[:, g, outputs].bitcast(FP8X4),
+                            lhsT_scale=wo_scales[:, g, outputs],
+                            rhs=attn_codes[:, b, n, g, :].bitcast(FP8X4),
+                            rhs_scale=attn_scales[:, b, n, g, :],
+                            start=(g == 0),
+                            stop=(g == PASSES - 1),
+                        )
+                for k in range(PACK):
+                    m = h * PACK + k
+                    nc.scalar.activation(
+                        out=y_turned[:, m, :], in_=bank[:, k, :], func=ACT.Identity, bias=bo_cols[:, m : m + 1]
+                    )
+            return y_turned
+
+        def residual(i, y_turned):
+            b, n = divmod(i, T_BLOCKS)
+            x = [psum_x.tile([P, BANK], F32, name="x") for h in range(O_BANKS)]
+            for h in range(O_BANKS):
+                nc.tensor.matmul(
+                    x[h][:],
+                    lhsT=ident_bf[:],
+                    rhs=audio_raw[b][:, n, h * BANK : (h + 1) * BANK],
+                    start=True,
+                    stop=False,
+                )
+                for k in range(PACK):
+                    nc.tensor.matmul(
+                        x[h][:, k * P : (k + 1) * P],
+                        lhsT=y_turned[:, h * PACK + k, :],
+                        rhs=ident[:],
+                        is_transpose=True,
+                        start=False,
+                        stop=(k == PACK - 1),
+                    )
             return x
 
-        def project(i, x):
-            b, n = divmod(i, T_BLOCKS)
-            y = [psum_y.tile([P, BANK], F32, name="y") for h in range(O_BANKS)]
-            sums = small.tile([P, O_BANKS], F32)
+        def statistics(x):
+            stats = small.tile([P, O_BANKS, 6], F32)
             for h in range(O_BANKS):
-                outputs = slice(h * BANK, (h + 1) * BANK)
-                for g in range(PASSES):
-                    nc.tensor.matmul_mx(
-                        out=y[h][:],
-                        lhsT=attn_codes[:, b, n, g, :].bitcast(FP8X4),
-                        lhsT_scale=attn_scales[:, b, n, g, :],
-                        rhs=wo_codes[:, g, outputs].bitcast(FP8X4),
-                        rhs_scale=wo_scales[:, g, outputs],
-                        start=(g == 0),
-                        stop=(g == PASSES - 1),
-                    )
-            for h in range(O_BANKS):
-                outputs = slice(h * BANK, (h + 1) * BANK)
-                nc.vector.scalar_tensor_tensor(
-                    out=x[:, outputs],
-                    in0=y[h][:],
-                    scalar=1.0,
-                    in1=x[:, outputs],
-                    op0=ALU.mult,
-                    op1=ALU.add,
-                    accum_out=sums[:, h : h + 1],
-                )
-            scaled_sums = small.tile([P, O_BANKS], F32)
-            neg_mean = small.tile([P, 1], F32)
-            nc.scalar.activation(
-                out=scaled_sums[:], in_=sums[:], func=ACT.Identity, scale=-1.0 / D, accum_out=neg_mean[:, 0:1]
-            )
-            squares = stage.tile([P, D], BF16)
-            sum_squares = small.tile([P, 1], F32)
-            nc.scalar.activation(
-                out=squares[:], in_=x[:], func=ACT.Square, bias=neg_mean[:, 0:1], accum_out=sum_squares[:, 0:1]
-            )
+                nc.vector.bn_stats(out=stats[:, h, :], in_=x[h][:])
+            return stats
+
+        def mean_and_variance(stats):
+            mean_var = small.tile([P, 2], F32)
+            nc.vector.bn_aggr(out=mean_var[:], in_=stats[:].rearrange("p h s -> p (h s)"))
+            return mean_var
+
+        def deviation(mean_var):
             rstd = small.tile([P, 1], F32)
             nc.scalar.activation(
-                out=rstd[:], in_=sum_squares[:], func=ACT.Abs_reciprocal_sqrt, scale=1.0 / D, bias=eps_ln[:, 0:1]
+                out=rstd[:], in_=mean_var[:, 1:2], func=ACT.Abs_reciprocal_sqrt, scale=1.0, bias=eps_ln[:, 0:1]
             )
-            return neg_mean, rstd
+            return rstd
 
-        def centre_and_scale(x, neg_mean):
-            nc.vector.scalar_tensor_tensor(
-                out=x[:], in0=x[:], scalar=neg_mean[:, 0:1], in1=gamma_all[:], op0=ALU.add, op1=ALU.mult
-            )
+        def centre_and_scale(x, mean_var):
+            z = rows.tile([P, D], F32)
+            for h in range(O_BANKS):
+                outputs = slice(h * BANK, (h + 1) * BANK)
+                nc.vector.scalar_tensor_tensor(
+                    out=z[:, outputs],
+                    in0=x[h][:],
+                    scalar=mean_var[:, 0:1],
+                    in1=gamma_all[:, outputs],
+                    op0=ALU.subtract,
+                    op1=ALU.mult,
+                )
+            return z
 
-        def shift_and_store(i, x, rstd):
+        def shift_and_store(i, z, rstd):
             b, n = divmod(i, T_BLOCKS)
-            if 1 <= i < N_BLOCKS - 3:
-                nc.scalar.activation(out=x[:], in_=x[:], func=ACT.Copy, scale=rstd[:, 0:1])
-                nc.gpsimd.tensor_tensor(out=x[:], in0=x[:], in1=beta_sbuf[:], op=ALU.add)
-                nc.sync.dma_start(out=out[b, n * P : (n + 1) * P, :], in_=x[:])
+            if i < N_BLOCKS - N_VEC:
+                nc.scalar.activation(out=z[:], in_=z[:], func=ACT.Copy, scale=rstd[:, 0:1])
+                for h in range(O_BANKS):
+                    outputs = slice(h * BANK, (h + 1) * BANK)
+                    nc.gpsimd.tensor_tensor(out=z[:, outputs], in0=z[:, outputs], in1=beta_all[:, outputs], op=ALU.add)
             else:
                 nc.vector.scalar_tensor_tensor(
-                    out=x[:], in0=x[:], scalar=rstd[:, 0:1], in1=beta_all[:], op0=ALU.mult, op1=ALU.add
+                    out=z[:], in0=z[:], scalar=rstd[:, 0:1], in1=beta_all[:], op0=ALU.mult, op1=ALU.add
                 )
-                nc.sync.dma_start(out=out[b, n * P : (n + 1) * P, :], in_=x[:])
+            nc.sync.dma_start(out=out[b, n * P : (n + 1) * P, :], in_=z[:])
 
         for n in range(T_BLOCKS):
             transpose_q(0, n)
@@ -255,71 +311,68 @@ def tile_linearattentionlayer_pb_kernel(tc, q_feat, kv, k_sum, audio, Wo, bo, ga
             out=ksum[:].rearrange("p b g j -> p (b g j)"),
             in_=ksum_bank[:, 0, 0:n_ksum_rows].bitcast(BF16),
         )
-
-        def spread(v, bank):
-            for h in range(O_BANKS):
-                outputs = slice(h * BANK, (h + 1) * BANK)
-                nc.tensor.matmul(bank[:, outputs], lhsT=pick[:, v, :], rhs=vector_rows[:, outputs], start=True, stop=True)
-
-        bo_bank = psum_y.tile([P, D], BF16, tag="y")
-        spread(0, bo_bank)
-        bo_all = const.tile([P, D], BF16)
-        gamma_all = psum_const.tile([P, D], BF16)
-        spread(1, gamma_all)
-        beta_all = psum_const.tile([P, D], BF16)
-        spread(2, beta_all)
-        beta_sbuf = const.tile([P, D], BF16)
-
-        kv_grouped0 = regroup_kv(kv_raw[0], nc.vector.tensor_copy)
-        kv_raw.append(load_kv(1, 1))
-        q_raw.append(load_tokens(q_feat[1]))
-        nc.sync.dma_start(out=wo_raw[:], in_=Wo.rearrange("(n p) d -> p n d", p=P))
-        audio_raw = [load_tokens(audio[0]), load_tokens(audio[1])]
-        kv_grouped1 = regroup_kv(kv_raw[1], nc.vector.tensor_copy)
-        quantise_kv(0, 0, kv_grouped0)
-        quantise_q(0)
-        quantise_kv(0, 1, kv_grouped1)
         recip0 = [recips.tile([P, PACK, T], F32, name="recip") for g in range(PASSES)]
-        for g in range(PASSES):
-            for u in range(HALVES):
-                reciprocals(0, g, u, recip0[g])
-        nc.scalar.copy(out=bo_all[:], in_=bo_bank[:])
-        nc.scalar.copy(out=beta_sbuf[:], in_=beta_all[:])
+        recip1 = [recips.tile([P, PACK, T], F32, name="recip") for g in range(PASSES)]
+        for h in range(2):
+            for g in range(PASSES):
+                reciprocals(0, h, g, recip0[g])
 
-        kv_grouped = []
+        kv_grouped0 = regroup_kv(kv_raw[0], 2)
+        kv_grouped1 = regroup_kv(kv_raw[1], 2)
+        quantise_kv(0, 0, kv_grouped0)
+        quantise_kv(0, 1, kv_grouped1)
+        quantise_q(0)
+        kv_grouped = [regroup_kv(kv_raw[PASSES], 2)]
+        kv_raw.append(load_kv(1, 1, 1))
+        audio_raw = [load_tokens(audio[0], 1)]
+        nc.sync.dma_start(out=gamma_all[:], in_=gamma.partition_broadcast(P))
+        audio_raw.append(load_tokens(audio[1], 1))
+        nc.sync.dma_start(out=beta_all[:], in_=beta.partition_broadcast(P))
+
+        bo_bank = psum_x.tile([P, D], BF16, tag="x")
+        nc.tensor.transpose(bo_bank[:, 0:P], bo_rows[:], ident_bf[:])
+        bo_cols = const.tile([P, CHUNKS], F32)
+        nc.vector.tensor_copy(out=bo_cols[:], in_=bo_bank[:, 0:CHUNKS])
+
         attn_blocks = []
         for n in range(T_BLOCKS):
-            if n < PASSES:
-                kv_grouped.append(regroup_kv(kv_raw[PASSES + n], nc.vector.tensor_copy))
-            else:
-                quantise_kv(1, n - PASSES, kv_grouped[n - PASSES])
             attn_blocks.append(attention_products(0, n, recip0))
-            if n > 0:
+            if n == 0:
+                for m in range(T_BLOCKS):
+                    transpose_wo(m)
+            else:
                 quantise_attention(0, n - 1, attn_blocks[n - 1])
-            transpose_q(1, n)
-            transpose_wo(2 * n)
-            transpose_wo(2 * n + 1)
         quantise_attention(0, T_BLOCKS - 1, attn_blocks[T_BLOCKS - 1])
+        for m in range(T_BLOCKS, CHUNKS):
+            transpose_wo(m)
+        for n in range(T_BLOCKS):
+            transpose_q(1, n)
         quantise_wo(0)
         quantise_wo(1)
-        x = [residual(i) for i in range(AHEAD)]
-        quantise_q(1)
 
-        recip1 = [recips.tile([P, PACK, T], F32, name="recip") for g in range(PASSES)]
-        reciprocals(1, 0, 0, recip1[0])
-        stats = []
-        for s in range(N_BLOCKS + 2):
-            if s + 1 < PASSES * HALVES:
-                reciprocals(1, (s + 1) // HALVES, (s + 1) % HALVES, recip1[(s + 1) // HALVES])
-            if s + AHEAD < N_BLOCKS:
-                x.append(residual(s + AHEAD))
+        y_turned, x, stats, mean_var, rstd, z = [], [], [], [], [], []
+        for s in range(N_BLOCKS + 3):
+            if s < 2 * PASSES:
+                reciprocals(1, s // PASSES, s % PASSES, recip1[s % PASSES])
             if s < N_BLOCKS:
-                stats.append(project(s, x[s]))
+                y_turned.append(project(s))
             if FIRST <= s < FIRST + T_BLOCKS:
                 attn_block = attention_products(1, s - FIRST, recip1)
-            if s >= 2:
-                shift_and_store(s - 2, x[s - 2], stats[s - 2][1])
+            if s == 0:
+                kv_grouped.append(regroup_kv(kv_raw[PASSES + 1], 1))
+                quantise_kv(1, 0, kv_grouped[0])
+                quantise_q(1)
+            if s == 1:
+                quantise_kv(1, 1, kv_grouped[1])
+            if 1 <= s <= N_BLOCKS:
+                x.append(residual(s - 1, y_turned[s - 1]))
+                stats.append(statistics(x[s - 1]))
             if FIRST <= s < FIRST + T_BLOCKS:
                 quantise_attention(1, s - FIRST, attn_block)
+            if 2 <= s <= N_BLOCKS + 1:
+                rstd.append(deviation(mean_var[s - 2]))
+                z.append(centre_and_scale(x[s - 2], mean_var[s - 2]))
             if 1 <= s <= N_BLOCKS:
-                centre_and_scale(x[s - 1], stats[s - 1][0])
+                mean_var.append(mean_and_variance(stats[s - 1]))
+            if s >= 3:
+                shift_and_store(s - 3, z[s - 3], rstd[s - 3])

@@ -62,7 +62,7 @@ def tile_linearattentionlayer_pb_kernel(tc, q_feat, kv, k_sum, audio, Wo, bo, ga
             for n in range(0, T_BLOCKS, step):
                 nc.sync.dma_start(
                     out=token_rows[:, n : n + step, :],
-                    in_=src[n * P : (n + step) * P, :].rearrange("(n p) d -> p n d", p=P),
+                    in_=src.rearrange("(p n) d -> p n d", n=T_BLOCKS)[:, n : n + step, :],
                 )
             return token_rows
 
@@ -85,18 +85,17 @@ def tile_linearattentionlayer_pb_kernel(tc, q_feat, kv, k_sum, audio, Wo, bo, ga
                         )
             return kv_rows
 
-        kv_raw = [load_kv(0, 0, 2)]
-        kv_raw.append(load_kv(0, 1, 2))
-        q_raw = [load_tokens(q_feat[0], T_BLOCKS)]
+        kv00 = load_kv(0, 0, 1)
+        q_raw = [load_tokens(q_feat[0], 2)]
         nc.sync.dma_start(out=ksum_rows[0:n_ksum_rows, :], in_=k_sum.rearrange("b (r c) -> (b r) c", c=PAIR * P))
-        kv_raw.append(load_kv(1, 0, 2))
+        kv01 = load_kv(0, 1, 1)
+        kv10 = load_kv(1, 0, 1)
         nc.sync.dma_start(out=bo_rows[0:CHUNKS, :], in_=bo.rearrange("(m p) -> m p", p=P))
         for n in range(0, CHUNKS, CHUNKS // 2):
             nc.sync.dma_start(
                 out=wo_raw[:, n : n + CHUNKS // 2, :],
                 in_=Wo[n * P : (n + CHUNKS // 2) * P, :].rearrange("(n p) d -> p n d", p=P),
             )
-
         q_raw.append(load_tokens(q_feat[1], 1))
 
         ident = const.tile([P, P], F32)
@@ -119,17 +118,17 @@ def tile_linearattentionlayer_pb_kernel(tc, q_feat, kv, k_sum, audio, Wo, bo, ga
         attn_codes = keep.tile([P, B, T_BLOCKS, PASSES, P], U32, align_bytes=64)
         attn_scales = keep.tile([P, B, T_BLOCKS, PASSES, P], U8, align_bytes=64)
 
-        def transpose_rows(src_rows, dst_words):
+        def transpose_rows(src_rows, dst_words, copy=nc.scalar.copy):
             bank = psum_x.tile([P, PACK, P], F32, tag="x")
             for w in range(PASSES * HALVES):
                 nc.tensor.transpose(bank[:, w, :], src_rows.bitcast(F32)[:, w * P : (w + 1) * P], ident[:])
-            nc.scalar.copy(out=dst_words, in_=bank[:].rearrange("p (g u) r -> p g r u", g=PASSES))
+            copy(out=dst_words, in_=bank[:].rearrange("p (g u) r -> p g r u", g=PASSES))
 
         def transpose_q(b, n):
             transpose_rows(q_raw[b][:, n, :], q_grouped[:].bitcast(F32)[:, b, :, n * P : (n + 1) * P, :])
 
-        def transpose_wo(n):
-            transpose_rows(wo_raw[:, n, :], wo_grouped[:].bitcast(F32)[:, :, n * P : (n + 1) * P, :])
+        def transpose_wo(n, copy=nc.scalar.copy):
+            transpose_rows(wo_raw[:, n, :], wo_grouped[:].bitcast(F32)[:, :, n * P : (n + 1) * P, :], copy)
 
         def quantise_q(b):
             nc.vector.quantize_mx(
@@ -145,14 +144,27 @@ def tile_linearattentionlayer_pb_kernel(tc, q_feat, kv, k_sum, audio, Wo, bo, ga
                 in_=wo_grouped[:, g].rearrange("p o j -> p (o j)"),
             )
 
-        def regroup_kv(kv_rows, pieces, on_scalar=()):
+        def regroup_kv(kv_rows, pieces):
             kv_grouped = grouped.tile([P, PAIR, D // PAIR, PACK], BF16, align_bytes=64)
             width = D // pieces
             for i in range(pieces):
-                copy = nc.scalar.copy if i in on_scalar else nc.vector.tensor_copy
-                copy(
+                nc.vector.tensor_copy(
                     out=kv_grouped[:, :, i * width // PAIR : (i + 1) * width // PAIR, :],
                     in_=kv_rows[:, :, i * width : (i + 1) * width].rearrange("p j (c e) -> p e c j", e=PAIR),
+                )
+            return kv_grouped
+
+        def regroup_on_gpsimd(kv_rows, pieces):
+            kv_grouped = grouped.tile([P, PAIR, D // PAIR, PACK], BF16, align_bytes=64)
+            width = D // pieces
+            for i in range(pieces):
+                nc.gpsimd.tensor_scalar(
+                    out=kv_grouped[:, :, i * width // PAIR : (i + 1) * width // PAIR, :],
+                    in0=kv_rows[:, :, i * width : (i + 1) * width].rearrange("p j (c e) -> p e c j", e=PAIR),
+                    scalar1=1.0,
+                    scalar2=0.0,
+                    op0=ALU.mult,
+                    op1=ALU.add,
                 )
             return kv_grouped
 
@@ -175,9 +187,9 @@ def tile_linearattentionlayer_pb_kernel(tc, q_feat, kv, k_sum, audio, Wo, bo, ga
                 )
             nc.scalar.activation(out=recip[:, :, tokens], in_=recip[:, :, tokens], func=ACT.Square)
 
-        def attention_products(b, n, recip):
+        def attention_products(b, n):
             tokens = slice(n * P, (n + 1) * P)
-            attn_grouped = stage.tile([P, PASSES, P, PACK], BF16, align_bytes=64)
+            nums = []
             for g_out in range(PASSES):
                 num = psum_bank.tile([P, PACK, P], F32, tag="bank")
                 for j in range(PACK):
@@ -194,9 +206,16 @@ def tile_linearattentionlayer_pb_kernel(tc, q_feat, kv, k_sum, audio, Wo, bo, ga
                             start=(g == 0),
                             stop=(g == PASSES - 1),
                         )
+                nums.append(num)
+            return nums
+
+        def divide(n, nums, recip):
+            tokens = slice(n * P, (n + 1) * P)
+            attn_grouped = stage.tile([P, PASSES, P, PACK], BF16, align_bytes=64)
+            for g_out in range(PASSES):
                 nc.vector.tensor_tensor(
                     out=attn_grouped[:, g_out],
-                    in0=num[:].rearrange("p j t -> p t j"),
+                    in0=nums[g_out][:].rearrange("p j t -> p t j"),
                     in1=recip[g_out][:, :, tokens].rearrange("p j t -> p t j"),
                     op=ALU.mult,
                 )
@@ -299,7 +318,7 @@ def tile_linearattentionlayer_pb_kernel(tc, q_feat, kv, k_sum, audio, Wo, bo, ga
                 nc.vector.scalar_tensor_tensor(
                     out=z[:], in0=z[:], scalar=rstd[:, 0:1], in1=beta_all[:], op0=ALU.mult, op1=ALU.add
                 )
-            nc.sync.dma_start(out=out[b, n * P : (n + 1) * P, :], in_=z[:])
+            nc.sync.dma_start(out=out[b].rearrange("(p n) d -> p n d", n=T_BLOCKS)[:, n, :], in_=z[:])
 
         for n in range(T_BLOCKS):
             transpose_q(0, n)
@@ -317,13 +336,13 @@ def tile_linearattentionlayer_pb_kernel(tc, q_feat, kv, k_sum, audio, Wo, bo, ga
             for g in range(PASSES):
                 reciprocals(0, h, g, recip0[g])
 
-        kv_grouped0 = regroup_kv(kv_raw[0], 2)
-        kv_grouped1 = regroup_kv(kv_raw[1], 2)
-        quantise_kv(0, 0, kv_grouped0)
-        quantise_kv(0, 1, kv_grouped1)
+        grouped00 = regroup_kv(kv00, 1)
+        quantise_kv(0, 0, grouped00)
+        grouped01 = regroup_kv(kv01, 1)
         quantise_q(0)
-        kv_grouped = [regroup_kv(kv_raw[PASSES], 2)]
-        kv_raw.append(load_kv(1, 1, 1))
+        quantise_kv(0, 1, grouped01)
+        grouped10 = regroup_kv(kv10, 1)
+        kv11 = load_kv(1, 1, 1)
         audio_raw = [load_tokens(audio[0], 1)]
         nc.sync.dma_start(out=gamma_all[:], in_=gamma.partition_broadcast(P))
         audio_raw.append(load_tokens(audio[1], 1))
@@ -335,44 +354,53 @@ def tile_linearattentionlayer_pb_kernel(tc, q_feat, kv, k_sum, audio, Wo, bo, ga
         nc.vector.tensor_copy(out=bo_cols[:], in_=bo_bank[:, 0:CHUNKS])
 
         attn_blocks = []
-        for n in range(T_BLOCKS):
-            attn_blocks.append(attention_products(0, n, recip0))
-            if n == 0:
-                for m in range(T_BLOCKS):
-                    transpose_wo(m)
-            else:
-                quantise_attention(0, n - 1, attn_blocks[n - 1])
-        quantise_attention(0, T_BLOCKS - 1, attn_blocks[T_BLOCKS - 1])
-        for m in range(T_BLOCKS, CHUNKS):
-            transpose_wo(m)
+        attn_blocks.append(divide(0, attention_products(0, 0), recip0))
+        transpose_wo(0)
+        transpose_wo(1)
+        attn_blocks.append(divide(1, attention_products(0, 1), recip0))
+        quantise_attention(0, 0, attn_blocks[0])
+        transpose_wo(2)
+        transpose_wo(3)
+        attn_blocks.append(divide(2, attention_products(0, 2), recip0))
+        quantise_attention(0, 1, attn_blocks[1])
+        transpose_wo(4)
+        transpose_wo(5)
+        attn_blocks.append(divide(3, attention_products(0, 3), recip0))
+        quantise_attention(0, 2, attn_blocks[2])
+        transpose_wo(6)
+        transpose_wo(7)
         for n in range(T_BLOCKS):
             transpose_q(1, n)
         quantise_wo(0)
+        quantise_attention(0, 3, attn_blocks[3])
         quantise_wo(1)
 
-        y_turned, x, stats, mean_var, rstd, z = [], [], [], [], [], []
+        y_turned, x, nums, rstd, z = [], [], [], [], []
         for s in range(N_BLOCKS + 3):
             if s < 2 * PASSES:
                 reciprocals(1, s // PASSES, s % PASSES, recip1[s % PASSES])
+            if FIRST < s <= FIRST + T_BLOCKS:
+                attn_block = divide(s - FIRST - 1, nums[s - FIRST - 1], recip1)
             if s < N_BLOCKS:
                 y_turned.append(project(s))
-            if FIRST <= s < FIRST + T_BLOCKS:
-                attn_block = attention_products(1, s - FIRST, recip1)
             if s == 0:
-                kv_grouped.append(regroup_kv(kv_raw[PASSES + 1], 1))
-                quantise_kv(1, 0, kv_grouped[0])
+                grouped11 = regroup_kv(kv11, 1)
+                quantise_kv(1, 0, grouped10)
                 quantise_q(1)
-            if s == 1:
-                quantise_kv(1, 1, kv_grouped[1])
+                quantise_kv(1, 1, grouped11)
+            if FIRST <= s < FIRST + T_BLOCKS:
+                nums.append(attention_products(1, s - FIRST))
             if 1 <= s <= N_BLOCKS:
                 x.append(residual(s - 1, y_turned[s - 1]))
-                stats.append(statistics(x[s - 1]))
-            if FIRST <= s < FIRST + T_BLOCKS:
-                quantise_attention(1, s - FIRST, attn_block)
             if 2 <= s <= N_BLOCKS + 1:
-                rstd.append(deviation(mean_var[s - 2]))
-                z.append(centre_and_scale(x[s - 2], mean_var[s - 2]))
-            if 1 <= s <= N_BLOCKS:
-                mean_var.append(mean_and_variance(stats[s - 1]))
-            if s >= 3:
+                stats = statistics(x[s - 2])
+            if FIRST < s <= FIRST + T_BLOCKS:
+                quantise_attention(1, s - FIRST - 1, attn_block)
+            if s >= 3 and s - 3 >= N_BLOCKS - N_VEC:
+                shift_and_store(s - 3, z[s - 3], rstd[s - 3])
+            if 2 <= s <= N_BLOCKS + 1:
+                mean_var = mean_and_variance(stats)
+                rstd.append(deviation(mean_var))
+                z.append(centre_and_scale(x[s - 2], mean_var))
+            if s >= 3 and s - 3 < N_BLOCKS - N_VEC:
                 shift_and_store(s - 3, z[s - 3], rstd[s - 3])

@@ -26,7 +26,8 @@ BANK = 512
 O_BANKS = D // BANK
 N_BLOCKS = B * T_BLOCKS
 T_HALF = T // 2
-FIRST = T_BLOCKS - 2
+X_BANKS = 4
+FIRST = 2
 N_VEC = 2
 FLOPS = 2 * (2 * B * T * D * D)
 
@@ -44,7 +45,7 @@ def tile_linearattentionlayer_pb_kernel(tc, q_feat, kv, k_sum, audio, Wo, bo, ga
         rows = stack.enter_context(tc.tile_pool(name="rows", bufs=5))
         small = stack.enter_context(tc.tile_pool(name="small", bufs=4))
         psum_bank = stack.enter_context(tc.psum_pool(name="psum_bank", bufs=4))
-        psum_x = stack.enter_context(tc.psum_pool(name="psum_x", bufs=4))
+        psum_x = stack.enter_context(tc.psum_pool(name="psum_x", bufs=X_BANKS))
         stack.enter_context(tc.manual_schedule())
 
         n_ksum_rows = B * D // (PAIR * P)
@@ -66,36 +67,29 @@ def tile_linearattentionlayer_pb_kernel(tc, q_feat, kv, k_sum, audio, Wo, bo, ga
                 )
             return token_rows
 
-        def load_kv(b, g, pieces):
+        def load_kv(b, g):
             kv_rows = raw.tile([P, PACK, D], BF16)
-            width = D // pieces
-            for i in range(pieces):
-                columns = slice(i * width, (i + 1) * width)
-                for u in range(HALVES) if pieces > 1 else range(1):
-                    rows_u = slice(g * K_PASS + u * PAIR * P, g * K_PASS + (u + 1) * PAIR * P)
-                    if pieces > 1:
-                        nc.sync.dma_start(
-                            out=kv_rows[:, u * PAIR : (u + 1) * PAIR, columns],
-                            in_=kv[b, rows_u, columns].rearrange("(p e) c -> p e c", p=P),
-                        )
-                    else:
-                        nc.sync.dma_start(
-                            out=kv_rows[:].rearrange("p (u e) c -> p u (e c)", u=HALVES),
-                            in_=kv[b, g * K_PASS : (g + 1) * K_PASS, :].rearrange("(u p e) c -> p u (e c)", u=HALVES, p=P),
-                        )
+            nc.sync.dma_start(
+                out=kv_rows[:].rearrange("p (u e) c -> p u (e c)", u=HALVES),
+                in_=kv[b, g * K_PASS : (g + 1) * K_PASS, :].rearrange("(u p e) c -> p u (e c)", u=HALVES, p=P),
+            )
             return kv_rows
 
-        kv00 = load_kv(0, 0, 1)
+        def load_wo(h):
+            chunks = slice(h * CHUNKS // 2, (h + 1) * CHUNKS // 2)
+            nc.sync.dma_start(
+                out=wo_raw[:, chunks, :],
+                in_=Wo[h * D // 2 : (h + 1) * D // 2, :].rearrange("(n p) d -> p n d", p=P),
+            )
+
+        kv_raw = [load_kv(0, 0)]
         q_raw = [load_tokens(q_feat[0], 2)]
         nc.sync.dma_start(out=ksum_rows[0:n_ksum_rows, :], in_=k_sum.rearrange("b (r c) -> (b r) c", c=PAIR * P))
-        kv01 = load_kv(0, 1, 1)
-        kv10 = load_kv(1, 0, 1)
+        kv_raw.append(load_kv(0, 1))
         nc.sync.dma_start(out=bo_rows[0:CHUNKS, :], in_=bo.rearrange("(m p) -> m p", p=P))
-        for n in range(0, CHUNKS, CHUNKS // 2):
-            nc.sync.dma_start(
-                out=wo_raw[:, n : n + CHUNKS // 2, :],
-                in_=Wo[n * P : (n + CHUNKS // 2) * P, :].rearrange("(n p) d -> p n d", p=P),
-            )
+        load_wo(0)
+        kv_raw.append(load_kv(1, 0))
+        load_wo(1)
         q_raw.append(load_tokens(q_feat[1], 1))
 
         ident = const.tile([P, P], F32)
@@ -118,17 +112,17 @@ def tile_linearattentionlayer_pb_kernel(tc, q_feat, kv, k_sum, audio, Wo, bo, ga
         attn_codes = keep.tile([P, B, T_BLOCKS, PASSES, P], U32, align_bytes=64)
         attn_scales = keep.tile([P, B, T_BLOCKS, PASSES, P], U8, align_bytes=64)
 
-        def transpose_rows(src_rows, dst_words, copy=nc.scalar.copy):
+        def transpose_rows(src_rows, dst_words):
             bank = psum_x.tile([P, PACK, P], F32, tag="x")
             for w in range(PASSES * HALVES):
                 nc.tensor.transpose(bank[:, w, :], src_rows.bitcast(F32)[:, w * P : (w + 1) * P], ident[:])
-            copy(out=dst_words, in_=bank[:].rearrange("p (g u) r -> p g r u", g=PASSES))
+            nc.scalar.copy(out=dst_words, in_=bank[:].rearrange("p (g u) r -> p g r u", g=PASSES))
 
         def transpose_q(b, n):
             transpose_rows(q_raw[b][:, n, :], q_grouped[:].bitcast(F32)[:, b, :, n * P : (n + 1) * P, :])
 
-        def transpose_wo(n, copy=nc.scalar.copy):
-            transpose_rows(wo_raw[:, n, :], wo_grouped[:].bitcast(F32)[:, :, n * P : (n + 1) * P, :], copy)
+        def transpose_wo(n):
+            transpose_rows(wo_raw[:, n, :], wo_grouped[:].bitcast(F32)[:, :, n * P : (n + 1) * P, :])
 
         def quantise_q(b):
             nc.vector.quantize_mx(
@@ -144,28 +138,9 @@ def tile_linearattentionlayer_pb_kernel(tc, q_feat, kv, k_sum, audio, Wo, bo, ga
                 in_=wo_grouped[:, g].rearrange("p o j -> p (o j)"),
             )
 
-        def regroup_kv(kv_rows, pieces):
+        def regroup_kv(kv_rows):
             kv_grouped = grouped.tile([P, PAIR, D // PAIR, PACK], BF16, align_bytes=64)
-            width = D // pieces
-            for i in range(pieces):
-                nc.vector.tensor_copy(
-                    out=kv_grouped[:, :, i * width // PAIR : (i + 1) * width // PAIR, :],
-                    in_=kv_rows[:, :, i * width : (i + 1) * width].rearrange("p j (c e) -> p e c j", e=PAIR),
-                )
-            return kv_grouped
-
-        def regroup_on_gpsimd(kv_rows, pieces):
-            kv_grouped = grouped.tile([P, PAIR, D // PAIR, PACK], BF16, align_bytes=64)
-            width = D // pieces
-            for i in range(pieces):
-                nc.gpsimd.tensor_scalar(
-                    out=kv_grouped[:, :, i * width // PAIR : (i + 1) * width // PAIR, :],
-                    in0=kv_rows[:, :, i * width : (i + 1) * width].rearrange("p j (c e) -> p e c j", e=PAIR),
-                    scalar1=1.0,
-                    scalar2=0.0,
-                    op0=ALU.mult,
-                    op1=ALU.add,
-                )
+            nc.vector.tensor_copy(out=kv_grouped[:], in_=kv_rows[:].rearrange("p j (c e) -> p e c j", e=PAIR))
             return kv_grouped
 
         def quantise_kv(b, g, kv_grouped):
@@ -314,11 +289,21 @@ def tile_linearattentionlayer_pb_kernel(tc, q_feat, kv, k_sum, audio, Wo, bo, ga
                 for h in range(O_BANKS):
                     outputs = slice(h * BANK, (h + 1) * BANK)
                     nc.gpsimd.tensor_tensor(out=z[:, outputs], in0=z[:, outputs], in1=beta_all[:, outputs], op=ALU.add)
+                nc.sync.dma_start(out=out[b].rearrange("(p n) d -> p n d", n=T_BLOCKS)[:, n, :], in_=z[:])
             else:
-                nc.vector.scalar_tensor_tensor(
-                    out=z[:], in0=z[:], scalar=rstd[:, 0:1], in1=beta_all[:], op0=ALU.mult, op1=ALU.add
-                )
-            nc.sync.dma_start(out=out[b].rearrange("(p n) d -> p n d", n=T_BLOCKS)[:, n, :], in_=z[:])
+                for h in range(O_BANKS):
+                    outputs = slice(h * BANK, (h + 1) * BANK)
+                    nc.vector.scalar_tensor_tensor(
+                        out=z[:, outputs],
+                        in0=z[:, outputs],
+                        scalar=rstd[:, 0:1],
+                        in1=beta_all[:, outputs],
+                        op0=ALU.mult,
+                        op1=ALU.add,
+                    )
+                    nc.sync.dma_start(
+                        out=out[b].rearrange("(p n) d -> p n d", n=T_BLOCKS)[:, n, outputs], in_=z[:, outputs]
+                    )
 
         for n in range(T_BLOCKS):
             transpose_q(0, n)
@@ -336,13 +321,12 @@ def tile_linearattentionlayer_pb_kernel(tc, q_feat, kv, k_sum, audio, Wo, bo, ga
             for g in range(PASSES):
                 reciprocals(0, h, g, recip0[g])
 
-        grouped00 = regroup_kv(kv00, 1)
-        quantise_kv(0, 0, grouped00)
-        grouped01 = regroup_kv(kv01, 1)
+        kv_grouped = regroup_kv(kv_raw[0])
+        quantise_kv(0, 0, kv_grouped)
+        kv_grouped = regroup_kv(kv_raw[1])
         quantise_q(0)
-        quantise_kv(0, 1, grouped01)
-        grouped10 = regroup_kv(kv10, 1)
-        kv11 = load_kv(1, 1, 1)
+        quantise_kv(0, 1, kv_grouped)
+        kv_raw.append(load_kv(1, 1))
         audio_raw = [load_tokens(audio[0], 1)]
         nc.sync.dma_start(out=gamma_all[:], in_=gamma.partition_broadcast(P))
         audio_raw.append(load_tokens(audio[1], 1))
@@ -353,54 +337,53 @@ def tile_linearattentionlayer_pb_kernel(tc, q_feat, kv, k_sum, audio, Wo, bo, ga
         bo_cols = const.tile([P, CHUNKS], F32)
         nc.vector.tensor_copy(out=bo_cols[:], in_=bo_bank[:, 0:CHUNKS])
 
+        kv_grouped10 = regroup_kv(kv_raw[2])
+        for n in range(X_BANKS):
+            transpose_wo(n)
         attn_blocks = []
-        attn_blocks.append(divide(0, attention_products(0, 0), recip0))
-        transpose_wo(0)
-        transpose_wo(1)
-        attn_blocks.append(divide(1, attention_products(0, 1), recip0))
-        quantise_attention(0, 0, attn_blocks[0])
-        transpose_wo(2)
-        transpose_wo(3)
-        attn_blocks.append(divide(2, attention_products(0, 2), recip0))
-        quantise_attention(0, 1, attn_blocks[1])
-        transpose_wo(4)
-        transpose_wo(5)
-        attn_blocks.append(divide(3, attention_products(0, 3), recip0))
-        quantise_attention(0, 2, attn_blocks[2])
-        transpose_wo(6)
-        transpose_wo(7)
         for n in range(T_BLOCKS):
-            transpose_q(1, n)
-        quantise_wo(0)
-        quantise_attention(0, 3, attn_blocks[3])
-        quantise_wo(1)
+            if n == T_BLOCKS - 1:
+                for m in range(X_BANKS, CHUNKS):
+                    transpose_wo(m)
+                quantise_attention(0, n - 1, attn_blocks[n - 1])
+                for m in range(T_BLOCKS):
+                    transpose_q(1, m)
+                for g in range(PASSES):
+                    quantise_wo(g)
+            attn_blocks.append(divide(n, attention_products(0, n), recip0))
+            if 0 < n < T_BLOCKS - 1:
+                quantise_attention(0, n - 1, attn_blocks[n - 1])
+        kv_grouped11 = regroup_kv(kv_raw[3])
+        quantise_attention(0, T_BLOCKS - 1, attn_blocks[T_BLOCKS - 1])
 
         y_turned, x, nums, rstd, z = [], [], [], [], []
         for s in range(N_BLOCKS + 3):
-            if s < 2 * PASSES:
-                reciprocals(1, s // PASSES, s % PASSES, recip1[s % PASSES])
-            if FIRST < s <= FIRST + T_BLOCKS:
-                attn_block = divide(s - FIRST - 1, nums[s - FIRST - 1], recip1)
+            k = s - FIRST - 1
+            if 0 <= s - 3 < N_BLOCKS - N_VEC:
+                shift_and_store(s - 3, z[s - 3], rstd[s - 3])
+            if 0 <= k < T_BLOCKS:
+                attn_block = divide(k, nums[k], recip1)
             if s < N_BLOCKS:
                 y_turned.append(project(s))
-            if s == 0:
-                grouped11 = regroup_kv(kv11, 1)
-                quantise_kv(1, 0, grouped10)
-                quantise_q(1)
-                quantise_kv(1, 1, grouped11)
-            if FIRST <= s < FIRST + T_BLOCKS:
+            if 0 <= s - FIRST < T_BLOCKS:
                 nums.append(attention_products(1, s - FIRST))
             if 1 <= s <= N_BLOCKS:
                 x.append(residual(s - 1, y_turned[s - 1]))
-            if 2 <= s <= N_BLOCKS + 1:
+            if s == 0:
+                quantise_kv(1, 0, kv_grouped10)
+                quantise_q(1)
+            if s == 1:
+                quantise_kv(1, 1, kv_grouped11)
+            if s < 2 * PASSES:
+                h, g = divmod(s, PASSES)
+                reciprocals(1, h, g, recip1[g])
+            if 0 <= s - 2 < N_BLOCKS:
                 stats = statistics(x[s - 2])
-            if FIRST < s <= FIRST + T_BLOCKS:
-                quantise_attention(1, s - FIRST - 1, attn_block)
-            if s >= 3 and s - 3 >= N_BLOCKS - N_VEC:
+            if 0 <= k < T_BLOCKS:
+                quantise_attention(1, k, attn_block)
+            if s - 3 >= N_BLOCKS - N_VEC:
                 shift_and_store(s - 3, z[s - 3], rstd[s - 3])
-            if 2 <= s <= N_BLOCKS + 1:
+            if 0 <= s - 2 < N_BLOCKS:
                 mean_var = mean_and_variance(stats)
                 rstd.append(deviation(mean_var))
                 z.append(centre_and_scale(x[s - 2], mean_var))
-            if s >= 3 and s - 3 < N_BLOCKS - N_VEC:
-                shift_and_store(s - 3, z[s - 3], rstd[s - 3])

@@ -150,7 +150,7 @@ def tile_linearattentionlayer_pb_kernel(tc, q_feat, kv, k_sum, audio, Wo, bo, ga
                 in_=kv_grouped[:].rearrange("p e c j -> p (e c j)"),
             )
 
-        def reciprocals(b, h, g, recip):
+        def inverse_roots(b, h, g, recip):
             tokens = slice(h * T_HALF, (h + 1) * T_HALF)
             for j in range(PACK):
                 nc.scalar.activation(
@@ -160,6 +160,9 @@ def tile_linearattentionlayer_pb_kernel(tc, q_feat, kv, k_sum, audio, Wo, bo, ga
                     scale=ksum[:, b, g, j : j + 1],
                     bias=eps_denom[:, 0:1],
                 )
+
+        def square(h, recip):
+            tokens = slice(h * T_HALF, (h + 1) * T_HALF)
             nc.scalar.activation(out=recip[:, :, tokens], in_=recip[:, :, tokens], func=ACT.Square)
 
         def attention_products(b, n):
@@ -319,7 +322,9 @@ def tile_linearattentionlayer_pb_kernel(tc, q_feat, kv, k_sum, audio, Wo, bo, ga
         recip1 = [recips.tile([P, PACK, T], F32, name="recip") for g in range(PASSES)]
         for h in range(2):
             for g in range(PASSES):
-                reciprocals(0, h, g, recip0[g])
+                inverse_roots(0, h, g, recip0[g])
+            for g in range(PASSES):
+                square(h, recip0[g])
 
         kv_grouped = regroup_kv(kv_raw[0])
         quantise_kv(0, 0, kv_grouped)
@@ -359,6 +364,9 @@ def tile_linearattentionlayer_pb_kernel(tc, q_feat, kv, k_sum, audio, Wo, bo, ga
         y_turned, x, nums, rstd, z = [], [], [], [], []
         for s in range(N_BLOCKS + 3):
             k = s - FIRST - 1
+            if s < 2 * PASSES:
+                h, g = divmod(s, PASSES)
+                inverse_roots(1, h, g, recip1[g])
             if 0 <= s - 3 < N_BLOCKS - N_VEC:
                 shift_and_store(s - 3, z[s - 3], rstd[s - 3])
             if 0 <= k < T_BLOCKS:
@@ -376,7 +384,7 @@ def tile_linearattentionlayer_pb_kernel(tc, q_feat, kv, k_sum, audio, Wo, bo, ga
                 quantise_kv(1, 1, kv_grouped11)
             if s < 2 * PASSES:
                 h, g = divmod(s, PASSES)
-                reciprocals(1, h, g, recip1[g])
+                square(h, recip1[g])
             if 0 <= s - 2 < N_BLOCKS:
                 stats = statistics(x[s - 2])
             if 0 <= k < T_BLOCKS:

@@ -28,6 +28,7 @@ N_BLOCKS = B * T_BLOCKS
 T_HALF = T // 2
 X_BANKS = 4
 FIRST = 2
+SCALAR_STATS = (7,)
 N_VEC = 2
 FLOPS = 2 * (2 * B * T * D * D)
 
@@ -57,14 +58,15 @@ def tile_linearattentionlayer_pb_kernel(tc, q_feat, kv, k_sum, audio, Wo, bo, ga
         gamma_all = const.tile([P, D], BF16)
         beta_all = const.tile([P, D], BF16)
 
-        def load_tokens(src, pieces):
+        def load_blocks(token_rows, src, first, last):
+            nc.sync.dma_start(
+                out=token_rows[:, first:last, :],
+                in_=src.rearrange("(p n) d -> p n d", n=T_BLOCKS)[:, first:last, :],
+            )
+
+        def load_tokens(src):
             token_rows = raw.tile([P, T_BLOCKS, D], BF16)
-            step = T_BLOCKS // pieces
-            for n in range(0, T_BLOCKS, step):
-                nc.sync.dma_start(
-                    out=token_rows[:, n : n + step, :],
-                    in_=src.rearrange("(p n) d -> p n d", n=T_BLOCKS)[:, n : n + step, :],
-                )
+            load_blocks(token_rows, src, 0, T_BLOCKS)
             return token_rows
 
         def load_kv(b, g):
@@ -83,14 +85,16 @@ def tile_linearattentionlayer_pb_kernel(tc, q_feat, kv, k_sum, audio, Wo, bo, ga
             )
 
         kv_raw = [load_kv(0, 0)]
-        q_raw = [load_tokens(q_feat[0], 2)]
+        q_raw = [raw.tile([P, T_BLOCKS, D], BF16, name="token_rows")]
+        load_blocks(q_raw[0], q_feat[0], 0, T_BLOCKS // 2)
         nc.sync.dma_start(out=ksum_rows[0:n_ksum_rows, :], in_=k_sum.rearrange("b (r c) -> (b r) c", c=PAIR * P))
         kv_raw.append(load_kv(0, 1))
+        load_blocks(q_raw[0], q_feat[0], T_BLOCKS // 2, T_BLOCKS)
         nc.sync.dma_start(out=bo_rows[0:CHUNKS, :], in_=bo.rearrange("(m p) -> m p", p=P))
         load_wo(0)
         kv_raw.append(load_kv(1, 0))
         load_wo(1)
-        q_raw.append(load_tokens(q_feat[1], 1))
+        q_raw.append(load_tokens(q_feat[1]))
 
         ident = const.tile([P, P], F32)
         make_identity(nc, ident[:])
@@ -112,17 +116,18 @@ def tile_linearattentionlayer_pb_kernel(tc, q_feat, kv, k_sum, audio, Wo, bo, ga
         attn_codes = keep.tile([P, B, T_BLOCKS, PASSES, P], U32, align_bytes=64)
         attn_scales = keep.tile([P, B, T_BLOCKS, PASSES, P], U8, align_bytes=64)
 
-        def transpose_rows(src_rows, dst_words):
+        def transpose_rows(src_rows, dst_words, copy=nc.scalar.copy):
             bank = psum_x.tile([P, PACK, P], F32, tag="x")
             for w in range(PASSES * HALVES):
                 nc.tensor.transpose(bank[:, w, :], src_rows.bitcast(F32)[:, w * P : (w + 1) * P], ident[:])
-            nc.scalar.copy(out=dst_words, in_=bank[:].rearrange("p (g u) r -> p g r u", g=PASSES))
+            copy(out=dst_words, in_=bank[:].rearrange("p (g u) r -> p g r u", g=PASSES))
 
         def transpose_q(b, n):
             transpose_rows(q_raw[b][:, n, :], q_grouped[:].bitcast(F32)[:, b, :, n * P : (n + 1) * P, :])
 
         def transpose_wo(n):
-            transpose_rows(wo_raw[:, n, :], wo_grouped[:].bitcast(F32)[:, :, n * P : (n + 1) * P, :])
+            copy = nc.vector.tensor_copy if n >= CHUNKS - 2 else nc.scalar.copy
+            transpose_rows(wo_raw[:, n, :], wo_grouped[:].bitcast(F32)[:, :, n * P : (n + 1) * P, :], copy)
 
         def quantise_q(b):
             nc.vector.quantize_mx(
@@ -190,7 +195,7 @@ def tile_linearattentionlayer_pb_kernel(tc, q_feat, kv, k_sum, audio, Wo, bo, ga
         def divide(n, nums, recip):
             tokens = slice(n * P, (n + 1) * P)
             attn_grouped = stage.tile([P, PASSES, P, PACK], BF16, align_bytes=64)
-            for g_out in range(PASSES):
+            for g_out in reversed(range(PASSES)):
                 nc.vector.tensor_tensor(
                     out=attn_grouped[:, g_out],
                     in0=nums[g_out][:].rearrange("p j t -> p t j"),
@@ -255,7 +260,7 @@ def tile_linearattentionlayer_pb_kernel(tc, q_feat, kv, k_sum, audio, Wo, bo, ga
 
         def statistics(x):
             stats = small.tile([P, O_BANKS, 6], F32)
-            for h in range(O_BANKS):
+            for h in reversed(range(O_BANKS)):
                 nc.vector.bn_stats(out=stats[:, h, :], in_=x[h][:])
             return stats
 
@@ -264,28 +269,55 @@ def tile_linearattentionlayer_pb_kernel(tc, q_feat, kv, k_sum, audio, Wo, bo, ga
             nc.vector.bn_aggr(out=mean_var[:], in_=stats[:].rearrange("p h s -> p (h s)"))
             return mean_var
 
-        def deviation(mean_var):
+        def statistics_on_scalar(x):
+            sums = small.tile([P, O_BANKS], F32)
+            for h in range(O_BANKS):
+                unused = stage.tile([P, BANK], BF16)
+                nc.scalar.activation(out=unused[:], in_=x[h][:], func=ACT.Identity, accum_out=sums[:, h : h + 1])
+            scaled_sums = small.tile([P, O_BANKS], F32)
+            neg_mean = small.tile([P, 1], F32)
+            nc.scalar.activation(
+                out=scaled_sums[:], in_=sums[:], func=ACT.Identity, scale=-1.0 / D, accum_out=neg_mean[:, 0:1]
+            )
+            sum_squares = small.tile([P, O_BANKS], F32)
+            for h in range(O_BANKS):
+                unused = stage.tile([P, BANK], BF16)
+                nc.scalar.activation(
+                    out=unused[:],
+                    in_=x[h][:],
+                    func=ACT.Square,
+                    bias=neg_mean[:, 0:1],
+                    accum_out=sum_squares[:, h : h + 1],
+                )
+            scaled_squares = small.tile([P, O_BANKS], F32)
+            variance = small.tile([P, 1], F32)
+            nc.scalar.activation(
+                out=scaled_squares[:], in_=sum_squares[:], func=ACT.Identity, scale=1.0 / D, accum_out=variance[:, 0:1]
+            )
+            return neg_mean[:, 0:1], variance[:, 0:1]
+
+        def deviation(variance):
             rstd = small.tile([P, 1], F32)
             nc.scalar.activation(
-                out=rstd[:], in_=mean_var[:, 1:2], func=ACT.Abs_reciprocal_sqrt, scale=1.0, bias=eps_ln[:, 0:1]
+                out=rstd[:], in_=variance, func=ACT.Abs_reciprocal_sqrt, scale=1.0, bias=eps_ln[:, 0:1]
             )
             return rstd
 
-        def centre_and_scale(x, mean_var):
+        def centre_and_scale(x, mean, op):
             z = rows.tile([P, D], F32)
             for h in range(O_BANKS):
                 outputs = slice(h * BANK, (h + 1) * BANK)
                 nc.vector.scalar_tensor_tensor(
                     out=z[:, outputs],
                     in0=x[h][:],
-                    scalar=mean_var[:, 0:1],
+                    scalar=mean,
                     in1=gamma_all[:, outputs],
-                    op0=ALU.subtract,
+                    op0=op,
                     op1=ALU.mult,
                 )
             return z
 
-        def shift_and_store(i, z, rstd):
+        def shift_and_store(i, z, rstd, beta_psum=None):
             b, n = divmod(i, T_BLOCKS)
             if i < N_BLOCKS - N_VEC:
                 nc.scalar.activation(out=z[:], in_=z[:], func=ACT.Copy, scale=rstd[:, 0:1])
@@ -300,7 +332,7 @@ def tile_linearattentionlayer_pb_kernel(tc, q_feat, kv, k_sum, audio, Wo, bo, ga
                         out=z[:, outputs],
                         in0=z[:, outputs],
                         scalar=rstd[:, 0:1],
-                        in1=beta_all[:, outputs],
+                        in1=beta_psum[:, outputs],
                         op0=ALU.mult,
                         op1=ALU.add,
                     )
@@ -308,9 +340,10 @@ def tile_linearattentionlayer_pb_kernel(tc, q_feat, kv, k_sum, audio, Wo, bo, ga
                         out=out[b].rearrange("(p n) d -> p n d", n=T_BLOCKS)[:, n, outputs], in_=z[:, outputs]
                     )
 
-        for n in range(T_BLOCKS):
+        recip0 = [recips.tile([P, PACK, T], F32, name="recip") for g in range(PASSES)]
+        recip1 = [recips.tile([P, PACK, T], F32, name="recip") for g in range(PASSES)]
+        for n in range(T_BLOCKS // 2):
             transpose_q(0, n)
-
         ksum_bank = psum_bank.tile([P, PACK, P], F32, tag="bank")
         nc.tensor.transpose(ksum_bank[:, 0, :], ksum_rows[:].bitcast(F32), ident[:])
         ksum = const.tile([P, B, PASSES, PACK], F32)
@@ -318,23 +351,26 @@ def tile_linearattentionlayer_pb_kernel(tc, q_feat, kv, k_sum, audio, Wo, bo, ga
             out=ksum[:].rearrange("p b g j -> p (b g j)"),
             in_=ksum_bank[:, 0, 0:n_ksum_rows].bitcast(BF16),
         )
-        recip0 = [recips.tile([P, PACK, T], F32, name="recip") for g in range(PASSES)]
-        recip1 = [recips.tile([P, PACK, T], F32, name="recip") for g in range(PASSES)]
-        for h in range(2):
-            for g in range(PASSES):
-                inverse_roots(0, h, g, recip0[g])
-            for g in range(PASSES):
-                square(h, recip0[g])
+        for g in range(PASSES):
+            inverse_roots(0, 0, g, recip0[g])
+        for n in range(T_BLOCKS // 2, T_BLOCKS):
+            transpose_q(0, n)
+        for g in range(PASSES):
+            square(0, recip0[g])
+        for g in range(PASSES):
+            inverse_roots(0, 1, g, recip0[g])
+        for g in range(PASSES):
+            square(1, recip0[g])
 
         kv_grouped = regroup_kv(kv_raw[0])
         quantise_kv(0, 0, kv_grouped)
         kv_grouped = regroup_kv(kv_raw[1])
-        quantise_q(0)
         quantise_kv(0, 1, kv_grouped)
+        quantise_q(0)
         kv_raw.append(load_kv(1, 1))
-        audio_raw = [load_tokens(audio[0], 1)]
+        audio_raw = [load_tokens(audio[0])]
         nc.sync.dma_start(out=gamma_all[:], in_=gamma.partition_broadcast(P))
-        audio_raw.append(load_tokens(audio[1], 1))
+        audio_raw.append(load_tokens(audio[1]))
         nc.sync.dma_start(out=beta_all[:], in_=beta.partition_broadcast(P))
 
         bo_bank = psum_x.tile([P, D], BF16, tag="x")
@@ -385,13 +421,25 @@ def tile_linearattentionlayer_pb_kernel(tc, q_feat, kv, k_sum, audio, Wo, bo, ga
             if s < 2 * PASSES:
                 h, g = divmod(s, PASSES)
                 square(h, recip1[g])
-            if 0 <= s - 2 < N_BLOCKS:
+            if s - 2 in SCALAR_STATS:
+                neg_mean, variance = statistics_on_scalar(x[s - 2])
+            elif 0 <= s - 2 < N_BLOCKS:
                 stats = statistics(x[s - 2])
             if 0 <= k < T_BLOCKS:
                 quantise_attention(1, k, attn_block)
+            if s == N_BLOCKS + 3 - N_VEC - 1:
+                beta_psum = psum_bank.tile([P, D], BF16, tag="bank")
+                for half in range(O_BANKS):
+                    outputs = slice(half * BANK, (half + 1) * BANK)
+                    nc.tensor.matmul(
+                        beta_psum[:, outputs], lhsT=ident_bf[:], rhs=beta_all[:, outputs], start=True, stop=True
+                    )
             if s - 3 >= N_BLOCKS - N_VEC:
-                shift_and_store(s - 3, z[s - 3], rstd[s - 3])
-            if 0 <= s - 2 < N_BLOCKS:
+                shift_and_store(s - 3, z[s - 3], rstd[s - 3], beta_psum)
+            if s - 2 in SCALAR_STATS:
+                rstd.append(deviation(variance))
+                z.append(centre_and_scale(x[s - 2], neg_mean, ALU.add))
+            elif 0 <= s - 2 < N_BLOCKS:
                 mean_var = mean_and_variance(stats)
-                rstd.append(deviation(mean_var))
-                z.append(centre_and_scale(x[s - 2], mean_var))
+                rstd.append(deviation(mean_var[:, 1:2]))
+                z.append(centre_and_scale(x[s - 2], mean_var[:, 0:1], ALU.subtract))

@@ -29,6 +29,7 @@ T_HALF = T // 2
 X_BANKS = 4
 FIRST = 2
 SCALAR_STATS = (7,)
+SHARED = range(2, 4)
 N_VEC = 2
 FLOPS = 2 * (2 * B * T * D * D)
 
@@ -126,7 +127,7 @@ def tile_linearattentionlayer_pb_kernel(tc, q_feat, kv, k_sum, audio, Wo, bo, ga
             transpose_rows(q_raw[b][:, n, :], q_grouped[:].bitcast(F32)[:, b, :, n * P : (n + 1) * P, :])
 
         def transpose_wo(n):
-            copy = nc.vector.tensor_copy if n >= CHUNKS - 2 else nc.scalar.copy
+            copy = nc.vector.tensor_copy if n >= CHUNKS - 1 else nc.scalar.copy
             transpose_rows(wo_raw[:, n, :], wo_grouped[:].bitcast(F32)[:, :, n * P : (n + 1) * P, :], copy)
 
         def quantise_q(b):
@@ -303,9 +304,9 @@ def tile_linearattentionlayer_pb_kernel(tc, q_feat, kv, k_sum, audio, Wo, bo, ga
             )
             return rstd
 
-        def centre_and_scale(x, mean, op):
+        def centre_and_scale(x, mean, op, halves=O_BANKS):
             z = rows.tile([P, D], F32)
-            for h in range(O_BANKS):
+            for h in range(halves):
                 outputs = slice(h * BANK, (h + 1) * BANK)
                 nc.vector.scalar_tensor_tensor(
                     out=z[:, outputs],
@@ -316,6 +317,21 @@ def tile_linearattentionlayer_pb_kernel(tc, q_feat, kv, k_sum, audio, Wo, bo, ga
                     op1=ALU.mult,
                 )
             return z
+
+        def finish_shared(i, x, z, mean_var, rstd):
+            b, n = divmod(i, T_BLOCKS)
+            neg_mean = small.tile([P, 1], F32)
+            nc.scalar.activation(out=neg_mean[:], in_=mean_var[:, 0:1], func=ACT.Copy, scale=-1.0)
+            nc.scalar.activation(out=z[:, 0:BANK], in_=z[:, 0:BANK], func=ACT.Copy, scale=rstd[:, 0:1])
+            shift = small.tile([P, 1], F32)
+            nc.scalar.activation(out=shift[:], in_=neg_mean[:], func=ACT.Copy, scale=rstd[:, 0:1])
+            nc.gpsimd.tensor_tensor(out=z[:, 0:BANK], in0=z[:, 0:BANK], in1=beta_all[:, 0:BANK], op=ALU.add)
+            nc.scalar.activation(
+                out=z[:, BANK:D], in_=x[1][:], func=ACT.Identity, scale=rstd[:, 0:1], bias=shift[:, 0:1]
+            )
+            for vector, op in ((gamma_all, ALU.mult), (beta_all, ALU.add)):
+                nc.gpsimd.tensor_tensor(out=z[:, BANK:D], in0=z[:, BANK:D], in1=vector[:, BANK:D], op=op)
+            nc.sync.dma_start(out=out[b].rearrange("(p n) d -> p n d", n=T_BLOCKS)[:, n, :], in_=z[:])
 
         def shift_and_store(i, z, rstd, beta_psum=None):
             b, n = divmod(i, T_BLOCKS)
@@ -397,13 +413,15 @@ def tile_linearattentionlayer_pb_kernel(tc, q_feat, kv, k_sum, audio, Wo, bo, ga
         kv_grouped11 = regroup_kv(kv_raw[3])
         quantise_attention(0, T_BLOCKS - 1, attn_blocks[T_BLOCKS - 1])
 
-        y_turned, x, nums, rstd, z = [], [], [], [], []
+        y_turned, x, nums, mean_vars, rstd, z = [], [], [], [], [], []
         for s in range(N_BLOCKS + 3):
             k = s - FIRST - 1
             if s < 2 * PASSES:
                 h, g = divmod(s, PASSES)
                 inverse_roots(1, h, g, recip1[g])
-            if 0 <= s - 3 < N_BLOCKS - N_VEC:
+            if s - 3 in SHARED:
+                finish_shared(s - 3, x[s - 3], z[s - 3], mean_vars[s - 3], rstd[s - 3])
+            elif 0 <= s - 3 < N_BLOCKS - N_VEC:
                 shift_and_store(s - 3, z[s - 3], rstd[s - 3])
             if 0 <= k < T_BLOCKS:
                 attn_block = divide(k, nums[k], recip1)
@@ -441,5 +459,6 @@ def tile_linearattentionlayer_pb_kernel(tc, q_feat, kv, k_sum, audio, Wo, bo, ga
                 z.append(centre_and_scale(x[s - 2], neg_mean, ALU.add))
             elif 0 <= s - 2 < N_BLOCKS:
                 mean_var = mean_and_variance(stats)
+                mean_vars.append(mean_var)
                 rstd.append(deviation(mean_var[:, 1:2]))
-                z.append(centre_and_scale(x[s - 2], mean_var[:, 0:1], ALU.subtract))
+                z.append(centre_and_scale(x[s - 2], mean_var[:, 0:1], ALU.subtract, 1 if s - 2 in SHARED else O_BANKS))

@@ -41,7 +41,8 @@ def tile_linearattentionlayer_pb_kernel(tc, q_feat, kv, k_sum, audio, Wo, bo, ga
         raw = stack.enter_context(tc.tile_pool(name="raw", bufs=3))
         keep = stack.enter_context(tc.tile_pool(name="keep", bufs=1))
         grouped = stack.enter_context(tc.tile_pool(name="grouped", bufs=2))
-        recips = stack.enter_context(tc.tile_pool(name="recips", bufs=4))
+        roots = stack.enter_context(tc.tile_pool(name="roots", bufs=2))
+        recips = stack.enter_context(tc.tile_pool(name="recips", bufs=3))
         stage = stack.enter_context(tc.tile_pool(name="stage", bufs=2))
         turned = stack.enter_context(tc.tile_pool(name="turned", bufs=3))
         rows = stack.enter_context(tc.tile_pool(name="rows", bufs=5))
@@ -156,20 +157,19 @@ def tile_linearattentionlayer_pb_kernel(tc, q_feat, kv, k_sum, audio, Wo, bo, ga
                 in_=kv_grouped[:].rearrange("p e c j -> p (e c j)"),
             )
 
-        def inverse_roots(b, h, g, recip):
+        def inverse_roots(b, h, g, root):
             tokens = slice(h * T_HALF, (h + 1) * T_HALF)
             for j in range(PACK):
                 nc.scalar.activation(
-                    out=recip[:, j, tokens],
+                    out=root[:, j, :],
                     in_=q_grouped[:, b, g, tokens, j],
                     func=ACT.Abs_reciprocal_sqrt,
                     scale=ksum[:, b, g, j : j + 1],
                     bias=eps_denom[:, 0:1],
                 )
 
-        def square(h, recip):
-            tokens = slice(h * T_HALF, (h + 1) * T_HALF)
-            nc.scalar.activation(out=recip[:, :, tokens], in_=recip[:, :, tokens], func=ACT.Square)
+        def square(root, recip):
+            nc.scalar.activation(out=recip, in_=root, func=ACT.Square)
 
         def attention_products(b, n):
             tokens = slice(n * P, (n + 1) * P)
@@ -193,14 +193,13 @@ def tile_linearattentionlayer_pb_kernel(tc, q_feat, kv, k_sum, audio, Wo, bo, ga
                 nums.append(num)
             return nums
 
-        def divide(n, nums, recip):
-            tokens = slice(n * P, (n + 1) * P)
+        def divide(nums, recip):
             attn_grouped = stage.tile([P, PASSES, P, PACK], BF16, align_bytes=64)
             for g_out in reversed(range(PASSES)):
                 nc.vector.tensor_tensor(
                     out=attn_grouped[:, g_out],
                     in0=nums[g_out][:].rearrange("p j t -> p t j"),
-                    in1=recip[g_out][:, :, tokens].rearrange("p j t -> p t j"),
+                    in1=recip[g_out],
                     op=ALU.mult,
                 )
             return attn_grouped
@@ -357,7 +356,6 @@ def tile_linearattentionlayer_pb_kernel(tc, q_feat, kv, k_sum, audio, Wo, bo, ga
                     )
 
         recip0 = [recips.tile([P, PACK, T], F32, name="recip") for g in range(PASSES)]
-        recip1 = [recips.tile([P, PACK, T], F32, name="recip") for g in range(PASSES)]
         for n in range(T_BLOCKS // 2):
             transpose_q(0, n)
         ksum_bank = psum_bank.tile([P, PACK, P], F32, tag="bank")
@@ -367,16 +365,15 @@ def tile_linearattentionlayer_pb_kernel(tc, q_feat, kv, k_sum, audio, Wo, bo, ga
             out=ksum[:].rearrange("p b g j -> p (b g j)"),
             in_=ksum_bank[:, 0, 0:n_ksum_rows].bitcast(BF16),
         )
-        for g in range(PASSES):
-            inverse_roots(0, 0, g, recip0[g])
-        for n in range(T_BLOCKS // 2, T_BLOCKS):
-            transpose_q(0, n)
-        for g in range(PASSES):
-            square(0, recip0[g])
-        for g in range(PASSES):
-            inverse_roots(0, 1, g, recip0[g])
-        for g in range(PASSES):
-            square(1, recip0[g])
+        for h in range(T // T_HALF):
+            half = [recip0[g][:, :, h * T_HALF : (h + 1) * T_HALF] for g in range(PASSES)]
+            for g in range(PASSES):
+                inverse_roots(0, h, g, half[g])
+            if h == 0:
+                for n in range(T_BLOCKS // 2, T_BLOCKS):
+                    transpose_q(0, n)
+            for g in range(PASSES):
+                square(half[g], half[g])
 
         kv_grouped = regroup_kv(kv_raw[0])
         quantise_kv(0, 0, kv_grouped)
@@ -407,24 +404,28 @@ def tile_linearattentionlayer_pb_kernel(tc, q_feat, kv, k_sum, audio, Wo, bo, ga
                     transpose_q(1, m)
                 for g in range(PASSES):
                     quantise_wo(g)
-            attn_blocks.append(divide(n, attention_products(0, n), recip0))
+            tokens = slice(n * P, (n + 1) * P)
+            recip = [recip0[g][:, :, tokens].rearrange("p j t -> p t j") for g in range(PASSES)]
+            attn_blocks.append(divide(attention_products(0, n), recip))
             if 0 < n < T_BLOCKS - 1:
                 quantise_attention(0, n - 1, attn_blocks[n - 1])
         kv_grouped11 = regroup_kv(kv_raw[3])
         quantise_attention(0, T_BLOCKS - 1, attn_blocks[T_BLOCKS - 1])
 
+        recip1 = [recips.tile([P, T, PACK], F32, name="recip") for g in range(PASSES)]
         y_turned, x, nums, mean_vars, rstd, z = [], [], [], [], [], []
         for s in range(N_BLOCKS + 3):
             k = s - FIRST - 1
             if s < 2 * PASSES:
                 h, g = divmod(s, PASSES)
-                inverse_roots(1, h, g, recip1[g])
+                root = roots.tile([P, PACK, T_HALF], F32)
+                inverse_roots(1, h, g, root[:])
             if s - 3 in SHARED:
                 finish_shared(s - 3, x[s - 3], z[s - 3], mean_vars[s - 3], rstd[s - 3])
             elif 0 <= s - 3 < N_BLOCKS - N_VEC:
                 shift_and_store(s - 3, z[s - 3], rstd[s - 3])
             if 0 <= k < T_BLOCKS:
-                attn_block = divide(k, nums[k], recip1)
+                attn_block = divide(nums[k], [recip1[g][:, k * P : (k + 1) * P, :] for g in range(PASSES)])
             if s < N_BLOCKS:
                 y_turned.append(project(s))
             if 0 <= s - FIRST < T_BLOCKS:
@@ -438,7 +439,7 @@ def tile_linearattentionlayer_pb_kernel(tc, q_feat, kv, k_sum, audio, Wo, bo, ga
                 quantise_kv(1, 1, kv_grouped11)
             if s < 2 * PASSES:
                 h, g = divmod(s, PASSES)
-                square(h, recip1[g])
+                square(root[:].rearrange("p j t -> p t j"), recip1[g][:, h * T_HALF : (h + 1) * T_HALF, :])
             if s - 2 in SCALAR_STATS:
                 neg_mean, variance = statistics_on_scalar(x[s - 2])
             elif 0 <= s - 2 < N_BLOCKS:

from contextlib import ExitStack

import concourse.mybir as mybir
from concourse.masks import make_identity

F32 = mybir.dt.float32
BF16 = mybir.dt.bfloat16
U32 = mybir.dt.uint32
U8 = mybir.dt.uint8
FP8X4 = mybir.dt.float8_e4m3fn_x4
ALU = mybir.AluOpType
ACT = mybir.ActivationFunctionType

B, T, D = 2, 512, 1024
EPS_DENOM = 1e-6
EPS_LN = 1e-5
P = 128
PACK = 4
PAIR = 2
HALVES = PACK // PAIR
K_PASS = P * PACK
PASSES = D // K_PASS
T_BLOCKS = T // P
CHUNKS = D // P
BANK = 512
O_BANKS = D // BANK
N_BLOCKS = B * T_BLOCKS
T_HALF = T // 2
X_BANKS = 4
FIRST = 2
SCALAR_STATS = (7,)
SHARED = range(2, 4)
N_VEC = 2
FLOPS = 2 * (2 * B * T * D * D)


def tile_linearattentionlayer_pb_kernel(tc, q_feat, kv, k_sum, audio, Wo, bo, gamma, beta, out):
    nc = tc.nc
    with ExitStack() as stack:
        const = stack.enter_context(tc.tile_pool(name="const", bufs=1))
        raw = stack.enter_context(tc.tile_pool(name="raw", bufs=3))
        keep = stack.enter_context(tc.tile_pool(name="keep", bufs=1))
        grouped = stack.enter_context(tc.tile_pool(name="grouped", bufs=2))
        roots = stack.enter_context(tc.tile_pool(name="roots", bufs=2))
        recips = stack.enter_context(tc.tile_pool(name="recips", bufs=3))
        stage = stack.enter_context(tc.tile_pool(name="stage", bufs=2))
        turned = stack.enter_context(tc.tile_pool(name="turned", bufs=3))
        rows = stack.enter_context(tc.tile_pool(name="rows", bufs=5))
        small = stack.enter_context(tc.tile_pool(name="small", bufs=4))
        psum_bank = stack.enter_context(tc.psum_pool(name="psum_bank", bufs=4))
        psum_x = stack.enter_context(tc.psum_pool(name="psum_x", bufs=X_BANKS))
        stack.enter_context(tc.manual_schedule())

        n_ksum_rows = B * D // (PAIR * P)
        ksum_rows = const.tile([P, PAIR * P], BF16)
        nc.vector.memset(ksum_rows[:], 0.0)
        bo_rows = const.tile([P, P], BF16)
        nc.vector.memset(bo_rows[:], 0.0)
        wo_raw = const.tile([P, CHUNKS, D], BF16)
        gamma_all = const.tile([P, D], BF16)
        beta_all = const.tile([P, D], BF16)

        def load_blocks(token_rows, src, first, last):
            nc.sync.dma_start(
                out=token_rows[:, first:last, :],
                in_=src.rearrange("(p n) d -> p n d", n=T_BLOCKS)[:, first:last, :],
            )

        def load_tokens(src):
            token_rows = raw.tile([P, T_BLOCKS, D], BF16)
            load_blocks(token_rows, src, 0, T_BLOCKS)
            return token_rows

        def load_kv(b, g):
            kv_rows = raw.tile([P, PACK, D], BF16)
            nc.sync.dma_start(
                out=kv_rows[:].rearrange("p (u e) c -> p u (e c)", u=HALVES),
                in_=kv[b, g * K_PASS : (g + 1) * K_PASS, :].rearrange("(u p e) c -> p u (e c)", u=HALVES, p=P),
            )
            return kv_rows

        def load_wo(h):
            chunks = slice(h * CHUNKS // 2, (h + 1) * CHUNKS // 2)
            nc.sync.dma_start(
                out=wo_raw[:, chunks, :],
                in_=Wo[h * D // 2 : (h + 1) * D // 2, :].rearrange("(n p) d -> p n d", p=P),
            )

        kv_raw = [load_kv(0, 0)]
        q_raw = [raw.tile([P, T_BLOCKS, D], BF16, name="token_rows")]
        load_blocks(q_raw[0], q_feat[0], 0, T_BLOCKS // 2)
        nc.sync.dma_start(out=ksum_rows[0:n_ksum_rows, :], in_=k_sum.rearrange("b (r c) -> (b r) c", c=PAIR * P))
        kv_raw.append(load_kv(0, 1))
        load_blocks(q_raw[0], q_feat[0], T_BLOCKS // 2, T_BLOCKS)
        nc.sync.dma_start(out=bo_rows[0:CHUNKS, :], in_=bo.rearrange("(m p) -> m p", p=P))
        load_wo(0)
        kv_raw.append(load_kv(1, 0))
        load_wo(1)
        q_raw.append(load_tokens(q_feat[1]))

        ident = const.tile([P, P], F32)
        make_identity(nc, ident[:])
        ident_bf = const.tile([P, P], BF16)
        make_identity(nc, ident_bf[:])
        eps_denom = const.tile([P, 1], F32)
        nc.vector.memset(eps_denom[:], EPS_DENOM)
        eps_ln = const.tile([P, 1], F32)
        nc.vector.memset(eps_ln[:], EPS_LN)

        q_grouped = keep.tile([P, B, PASSES, T, PACK], BF16, align_bytes=64)
        q_codes = keep.tile([P, B, PASSES, T], U32, align_bytes=64)
        q_scales = keep.tile([P, B, PASSES, T], U8, align_bytes=64)
        kv_codes = keep.tile([P, B, PASSES, D], U32, align_bytes=64)
        kv_scales = keep.tile([P, B, PASSES, D], U8, align_bytes=64)
        wo_grouped = keep.tile([P, PASSES, D, PACK], BF16, align_bytes=64)
        wo_codes = keep.tile([P, PASSES, D], U32, align_bytes=64)
        wo_scales = keep.tile([P, PASSES, D], U8, align_bytes=64)
        attn_codes = keep.tile([P, B, T_BLOCKS, PASSES, P], U32, align_bytes=64)
        attn_scales = keep.tile([P, B, T_BLOCKS, PASSES, P], U8, align_bytes=64)

        def transpose_rows(src_rows, dst_words, copy=nc.scalar.copy):
            bank = psum_x.tile([P, PACK, P], F32, tag="x")
            for w in range(PASSES * HALVES):
                nc.tensor.transpose(bank[:, w, :], src_rows.bitcast(F32)[:, w * P : (w + 1) * P], ident[:])
            copy(out=dst_words, in_=bank[:].rearrange("p (g u) r -> p g r u", g=PASSES))

        def transpose_q(b, n):
            transpose_rows(q_raw[b][:, n, :], q_grouped[:].bitcast(F32)[:, b, :, n * P : (n + 1) * P, :])

        def transpose_wo(n):
            copy = nc.vector.tensor_copy if n >= CHUNKS - 1 else nc.scalar.copy
            transpose_rows(wo_raw[:, n, :], wo_grouped[:].bitcast(F32)[:, :, n * P : (n + 1) * P, :], copy)

        def quantise_q(b):
            nc.vector.quantize_mx(
                out=q_codes[:, b].rearrange("p g t -> p (g t)").bitcast(FP8X4),
                scales=q_scales[:, b].rearrange("p g t -> p (g t)"),
                in_=q_grouped[:, b].rearrange("p g t j -> p (g t j)"),
            )

        def quantise_wo(g):
            nc.vector.quantize_mx(
                out=wo_codes[:, g, :].bitcast(FP8X4),
                scales=wo_scales[:, g, :],
                in_=wo_grouped[:, g].rearrange("p o j -> p (o j)"),
            )

        def regroup_kv(kv_rows):
            kv_grouped = grouped.tile([P, PAIR, D // PAIR, PACK], BF16, align_bytes=64)
            nc.vector.tensor_copy(out=kv_grouped[:], in_=kv_rows[:].rearrange("p j (c e) -> p e c j", e=PAIR))
            return kv_grouped

        def quantise_kv(b, g, kv_grouped):
            nc.vector.quantize_mx(
                out=kv_codes[:, b, g, :].bitcast(FP8X4),
                scales=kv_scales[:, b, g, :],
                in_=kv_grouped[:].rearrange("p e c j -> p (e c j)"),
            )

        def inverse_roots(b, h, g, root):
            tokens = slice(h * T_HALF, (h + 1) * T_HALF)
            for j in range(PACK):
                nc.scalar.activation(
                    out=root[:, j, :],
                    in_=q_grouped[:, b, g, tokens, j],
                    func=ACT.Abs_reciprocal_sqrt,
                    scale=ksum[:, b, g, j : j + 1],
                    bias=eps_denom[:, 0:1],
                )

        def square(root, recip):
            nc.scalar.activation(out=recip, in_=root, func=ACT.Square)

        def attention_products(b, n):
            tokens = slice(n * P, (n + 1) * P)
            nums = []
            for g_out in range(PASSES):
                num = psum_bank.tile([P, PACK, P], F32, tag="bank")
                for j in range(PACK):
                    u, e = divmod(j, PAIR)
                    first = e * (D // PAIR) + (g_out * HALVES + u) * P
                    features = slice(first, first + P)
                    for g in range(PASSES):
                        nc.tensor.matmul_mx(
                            out=num[:, j, :],
                            lhsT=kv_codes[:, b, g, features].bitcast(FP8X4),
                            lhsT_scale=kv_scales[:, b, g, features],
                            rhs=q_codes[:, b, g, tokens].bitcast(FP8X4),
                            rhs_scale=q_scales[:, b, g, tokens],
                            start=(g == 0),
                            stop=(g == PASSES - 1),
                        )
                nums.append(num)
            return nums

        def divide(nums, recip):
            attn_grouped = stage.tile([P, PASSES, P, PACK], BF16, align_bytes=64)
            for g_out in reversed(range(PASSES)):
                nc.vector.tensor_tensor(
                    out=attn_grouped[:, g_out],
                    in0=nums[g_out][:].rearrange("p j t -> p t j"),
                    in1=recip[g_out],
                    op=ALU.mult,
                )
            return attn_grouped

        def quantise_attention(b, n, attn_grouped):
            nc.vector.quantize_mx(
                out=attn_codes[:, b, n].rearrange("p g t -> p (g t)").bitcast(FP8X4),
                scales=attn_scales[:, b, n].rearrange("p g t -> p (g t)"),
                in_=attn_grouped[:].rearrange("p g t j -> p (g t j)"),
            )

        def project(i):
            b, n = divmod(i, T_BLOCKS)
            y_turned = turned.tile([P, CHUNKS, P], F32)
            for h in range(O_BANKS):
                bank = psum_bank.tile([P, PACK, P], F32, tag="bank")
                for k in range(PACK):
                    m = h * PACK + k
                    outputs = slice(m * P, (m + 1) * P)
                    for g in range(PASSES):
                        nc.tensor.matmul_mx(
                            out=bank[:, k, :],
                            lhsT=wo_codes[:, g, outputs].bitcast(FP8X4),
                            lhsT_scale=wo_scales[:, g, outputs],
                            rhs=attn_codes[:, b, n, g, :].bitcast(FP8X4),
                            rhs_scale=attn_scales[:, b, n, g, :],
                            start=(g == 0),
                            stop=(g == PASSES - 1),
                        )
                for k in range(PACK):
                    m = h * PACK + k
                    nc.scalar.activation(
                        out=y_turned[:, m, :], in_=bank[:, k, :], func=ACT.Identity, bias=bo_cols[:, m : m + 1]
                    )
            return y_turned

        def residual(i, y_turned):
            b, n = divmod(i, T_BLOCKS)
            x = [psum_x.tile([P, BANK], F32, name="x") for h in range(O_BANKS)]
            for h in range(O_BANKS):
                nc.tensor.matmul(
                    x[h][:],
                    lhsT=ident_bf[:],
                    rhs=audio_raw[b][:, n, h * BANK : (h + 1) * BANK],
                    start=True,
                    stop=False,
                )
                for k in range(PACK):
                    nc.tensor.matmul(
                        x[h][:, k * P : (k + 1) * P],
                        lhsT=y_turned[:, h * PACK + k, :],
                        rhs=ident[:],
                        is_transpose=True,
                        start=False,
                        stop=(k == PACK - 1),
                    )
            return x

        def statistics(x):
            stats = small.tile([P, O_BANKS, 6], F32)
            for h in reversed(range(O_BANKS)):
                nc.vector.bn_stats(out=stats[:, h, :], in_=x[h][:])
            return stats

        def mean_and_variance(stats):
            mean_var = small.tile([P, 2], F32)
            nc.vector.bn_aggr(out=mean_var[:], in_=stats[:].rearrange("p h s -> p (h s)"))
            return mean_var

        def statistics_on_scalar(x):
            sums = small.tile([P, O_BANKS], F32)
            for h in range(O_BANKS):
                unused = stage.tile([P, BANK], BF16)
                nc.scalar.activation(out=unused[:], in_=x[h][:], func=ACT.Identity, accum_out=sums[:, h : h + 1])
            scaled_sums = small.tile([P, O_BANKS], F32)
            neg_mean = small.tile([P, 1], F32)
            nc.scalar.activation(
                out=scaled_sums[:], in_=sums[:], func=ACT.Identity, scale=-1.0 / D, accum_out=neg_mean[:, 0:1]
            )
            sum_squares = small.tile([P, O_BANKS], F32)
            for h in range(O_BANKS):
                unused = stage.tile([P, BANK], BF16)
                nc.scalar.activation(
                    out=unused[:],
                    in_=x[h][:],
                    func=ACT.Square,
                    bias=neg_mean[:, 0:1],
                    accum_out=sum_squares[:, h : h + 1],
                )
            scaled_squares = small.tile([P, O_BANKS], F32)
            variance = small.tile([P, 1], F32)
            nc.scalar.activation(
                out=scaled_squares[:], in_=sum_squares[:], func=ACT.Identity, scale=1.0 / D, accum_out=variance[:, 0:1]
            )
            return neg_mean[:, 0:1], variance[:, 0:1]

        def deviation(variance):
            rstd = small.tile([P, 1], F32)
            nc.scalar.activation(
                out=rstd[:], in_=variance, func=ACT.Abs_reciprocal_sqrt, scale=1.0, bias=eps_ln[:, 0:1]
            )
            return rstd

        def centre_and_scale(x, mean, op, halves=O_BANKS):
            z = rows.tile([P, D], F32)
            for h in range(halves):
                outputs = slice(h * BANK, (h + 1) * BANK)
                nc.vector.scalar_tensor_tensor(
                    out=z[:, outputs],
                    in0=x[h][:],
                    scalar=mean,
                    in1=gamma_all[:, outputs],
                    op0=op,
                    op1=ALU.mult,
                )
            return z

        def finish_shared(i, x, z, mean_var, rstd):
            b, n = divmod(i, T_BLOCKS)
            neg_mean = small.tile([P, 1], F32)
            nc.scalar.activation(out=neg_mean[:], in_=mean_var[:, 0:1], func=ACT.Copy, scale=-1.0)
            nc.scalar.activation(out=z[:, 0:BANK], in_=z[:, 0:BANK], func=ACT.Copy, scale=rstd[:, 0:1])
            shift = small.tile([P, 1], F32)
            nc.scalar.activation(out=shift[:], in_=neg_mean[:], func=ACT.Copy, scale=rstd[:, 0:1])
            nc.gpsimd.tensor_tensor(out=z[:, 0:BANK], in0=z[:, 0:BANK], in1=beta_all[:, 0:BANK], op=ALU.add)
            nc.scalar.activation(
                out=z[:, BANK:D], in_=x[1][:], func=ACT.Identity, scale=rstd[:, 0:1], bias=shift[:, 0:1]
            )
            for vector, op in ((gamma_all, ALU.mult), (beta_all, ALU.add)):
                nc.gpsimd.tensor_tensor(out=z[:, BANK:D], in0=z[:, BANK:D], in1=vector[:, BANK:D], op=op)
            nc.sync.dma_start(out=out[b].rearrange("(p n) d -> p n d", n=T_BLOCKS)[:, n, :], in_=z[:])

        def shift_and_store(i, z, rstd, beta_psum=None):
            b, n = divmod(i, T_BLOCKS)
            if i < N_BLOCKS - N_VEC:
                nc.scalar.activation(out=z[:], in_=z[:], func=ACT.Copy, scale=rstd[:, 0:1])
                for h in range(O_BANKS):
                    outputs = slice(h * BANK, (h + 1) * BANK)
                    nc.gpsimd.tensor_tensor(out=z[:, outputs], in0=z[:, outputs], in1=beta_all[:, outputs], op=ALU.add)
                nc.sync.dma_start(out=out[b].rearrange("(p n) d -> p n d", n=T_BLOCKS)[:, n, :], in_=z[:])
            else:
                for h in range(O_BANKS):
                    outputs = slice(h * BANK, (h + 1) * BANK)
                    nc.vector.scalar_tensor_tensor(
                        out=z[:, outputs],
                        in0=z[:, outputs],
                        scalar=rstd[:, 0:1],
                        in1=beta_psum[:, outputs],
                        op0=ALU.mult,
                        op1=ALU.add,
                    )
                    nc.sync.dma_start(
                        out=out[b].rearrange("(p n) d -> p n d", n=T_BLOCKS)[:, n, outputs], in_=z[:, outputs]
                    )

        recip0 = [recips.tile([P, PACK, T], F32, name="recip") for g in range(PASSES)]
        for n in range(T_BLOCKS // 2):
            transpose_q(0, n)
        ksum_bank = psum_bank.tile([P, PACK, P], F32, tag="bank")
        nc.tensor.transpose(ksum_bank[:, 0, :], ksum_rows[:].bitcast(F32), ident[:])
        ksum = const.tile([P, B, PASSES, PACK], F32)
        nc.scalar.copy(
            out=ksum[:].rearrange("p b g j -> p (b g j)"),
            in_=ksum_bank[:, 0, 0:n_ksum_rows].bitcast(BF16),
        )
        for h in range(T // T_HALF):
            half = [recip0[g][:, :, h * T_HALF : (h + 1) * T_HALF] for g in range(PASSES)]
            for g in range(PASSES):
                inverse_roots(0, h, g, half[g])
            if h == 0:
                for n in range(T_BLOCKS // 2, T_BLOCKS):
                    transpose_q(0, n)
            for g in range(PASSES):
                square(half[g], half[g])

        kv_grouped = regroup_kv(kv_raw[0])
        quantise_kv(0, 0, kv_grouped)
        kv_grouped = regroup_kv(kv_raw[1])
        quantise_kv(0, 1, kv_grouped)
        quantise_q(0)
        kv_raw.append(load_kv(1, 1))
        audio_raw = [load_tokens(audio[0])]
        nc.sync.dma_start(out=gamma_all[:], in_=gamma.partition_broadcast(P))
        audio_raw.append(load_tokens(audio[1]))
        nc.sync.dma_start(out=beta_all[:], in_=beta.partition_broadcast(P))

        bo_bank = psum_x.tile([P, D], BF16, tag="x")
        nc.tensor.transpose(bo_bank[:, 0:P], bo_rows[:], ident_bf[:])
        bo_cols = const.tile([P, CHUNKS], F32)
        nc.vector.tensor_copy(out=bo_cols[:], in_=bo_bank[:, 0:CHUNKS])

        kv_grouped10 = regroup_kv(kv_raw[2])
        for n in range(X_BANKS):
            transpose_wo(n)
        attn_blocks = []
        for n in range(T_BLOCKS):
            if n == T_BLOCKS - 1:
                for m in range(X_BANKS, CHUNKS):
                    transpose_wo(m)
                quantise_attention(0, n - 1, attn_blocks[n - 1])
                for m in range(T_BLOCKS):
                    transpose_q(1, m)
                for g in range(PASSES):
                    quantise_wo(g)
            tokens = slice(n * P, (n + 1) * P)
            recip = [recip0[g][:, :, tokens].rearrange("p j t -> p t j") for g in range(PASSES)]
            attn_blocks.append(divide(attention_products(0, n), recip))
            if 0 < n < T_BLOCKS - 1:
                quantise_attention(0, n - 1, attn_blocks[n - 1])
        kv_grouped11 = regroup_kv(kv_raw[3])
        quantise_attention(0, T_BLOCKS - 1, attn_blocks[T_BLOCKS - 1])

        recip1 = [recips.tile([P, T, PACK], F32, name="recip") for g in range(PASSES)]
        y_turned, x, nums, mean_vars, rstd, z = [], [], [], [], [], []
        for s in range(N_BLOCKS + 3):
            k = s - FIRST - 1
            if s < 2 * PASSES:
                h, g = divmod(s, PASSES)
                root = roots.tile([P, PACK, T_HALF], F32)
                inverse_roots(1, h, g, root[:])
            if s - 3 in SHARED:
                finish_shared(s - 3, x[s - 3], z[s - 3], mean_vars[s - 3], rstd[s - 3])
            elif 0 <= s - 3 < N_BLOCKS - N_VEC:
                shift_and_store(s - 3, z[s - 3], rstd[s - 3])
            if 0 <= k < T_BLOCKS:
                attn_block = divide(nums[k], [recip1[g][:, k * P : (k + 1) * P, :] for g in range(PASSES)])
            if s < N_BLOCKS:
                y_turned.append(project(s))
            if 0 <= s - FIRST < T_BLOCKS:
                nums.append(attention_products(1, s - FIRST))
            if 1 <= s <= N_BLOCKS:
                x.append(residual(s - 1, y_turned[s - 1]))
            if s == 0:
                quantise_kv(1, 0, kv_grouped10)
                quantise_q(1)
            if s == 1:
                quantise_kv(1, 1, kv_grouped11)
            if s < 2 * PASSES:
                h, g = divmod(s, PASSES)
                square(root[:].rearrange("p j t -> p t j"), recip1[g][:, h * T_HALF : (h + 1) * T_HALF, :])
            if s - 2 in SCALAR_STATS:
                neg_mean, variance = statistics_on_scalar(x[s - 2])
            elif 0 <= s - 2 < N_BLOCKS:
                stats = statistics(x[s - 2])
            if 0 <= k < T_BLOCKS:
                quantise_attention(1, k, attn_block)
            if s == N_BLOCKS + 3 - N_VEC - 1:
                beta_psum = psum_bank.tile([P, D], BF16, tag="bank")
                for half in range(O_BANKS):
                    outputs = slice(half * BANK, (half + 1) * BANK)
                    nc.tensor.matmul(
                        beta_psum[:, outputs], lhsT=ident_bf[:], rhs=beta_all[:, outputs], start=True, stop=True
                    )
            if s - 3 >= N_BLOCKS - N_VEC:
                shift_and_store(s - 3, z[s - 3], rstd[s - 3], beta_psum)
            if s - 2 in SCALAR_STATS:
                rstd.append(deviation(variance))
                z.append(centre_and_scale(x[s - 2], neg_mean, ALU.add))
            elif 0 <= s - 2 < N_BLOCKS:
                mean_var = mean_and_variance(stats)
                mean_vars.append(mean_var)
                rstd.append(deviation(mean_var[:, 1:2]))
                z.append(centre_and_scale(x[s - 2], mean_var[:, 0:1], ALU.subtract, 1 if s - 2 in SHARED else O_BANKS))
